import numpy as np
import ml_dtypes


def mxq(x, axis, fmt="e4m3"):
    dtype, down = {"e4m3": (ml_dtypes.float8_e4m3fn, 7), "e5m2": (ml_dtypes.float8_e5m2, 14)}[fmt]
    v = np.moveaxis(np.asarray(x, np.float32).astype(ml_dtypes.bfloat16).astype(np.float64), axis, -1)
    blocks = v.reshape(v.shape[:-1] + (-1, 32))
    amax = np.abs(blocks).max(-1, keepdims=True)
    byte = np.maximum(np.where(amax > 0, np.frexp(amax)[1] - 1 + 127, 0) - down, 1)
    scale = np.exp2(byte - 127.0)
    codes = (blocks / scale).astype(np.float32).astype(dtype).astype(np.float64)
    return np.moveaxis((codes * scale).reshape(v.shape), -1, axis)


WIDE = False


def mx_kscale(k):
    if not WIDE:
        return np.ones(k)
    levels = np.array([10, -10, 5, -5, 0])
    if k % 512:
        return np.exp2(np.random.permutation(np.resize(levels, k // 32))).repeat(32)
    a = np.empty((k // 512, 16))
    for p in range(k // 512):
        a[p, :8] = np.random.permutation(np.resize(levels, 8))
        for g in range(8):
            far = levels[np.abs(levels - a[p, g]) >= 10]
            a[p, g + 8] = far[np.random.randint(len(far))]
    return np.exp2(a.ravel()).repeat(32)


BF16 = ml_dtypes.bfloat16


def bf(x):
    return np.asarray(x, np.float32).astype(BF16)


def f64(x):
    return np.asarray(x).astype(np.float64)


B, L, LV, H = 32, 32, 64, 1024
NUM_ITERATIONS = 3
X = 0.25
V = 0.12 * L
A = 0.6 / (np.sqrt(H) * V)


def setup_inputs():
    s = mx_kscale(H)
    return {"text_feat": bf(np.random.standard_normal((B, L, H)) * X * s),
            "vision_proj": bf(np.random.standard_normal((B, 1, H)) * V),
            "Wt": bf(np.random.standard_normal((H, H)) * A / (X * np.sqrt(H)) / s[None, :]),
            "bt": bf(np.random.standard_normal(H) * 0.5 * A)}


def reference(text_feat, vision_proj, Wt, bt):
    vp = f64(vision_proj)
    text_proj = (mxq(f64(text_feat), 2, "e4m3") @ mxq(f64(Wt), 1, "e4m3").T) + f64(bt)
    agreement = np.sum(text_proj * vp, axis=-1, keepdims=True)
    coupling = np.zeros_like(agreement)
    for _ in range(NUM_ITERATIONS - 1):
        coupling = coupling + agreement
    e = np.exp(coupling - coupling.max(axis=1, keepdims=True))
    routing_weights = e / e.sum(axis=1, keepdims=True)
    weighted_vision = routing_weights * vp
    return text_proj, weighted_vision

@@ -1,0 +1,289 @@
+from contextlib import ExitStack
+
+import concourse.mybir as mybir
+from concourse.masks import make_identity
+
+F32 = mybir.dt.float32
+BF16 = mybir.dt.bfloat16
+U32 = mybir.dt.uint32
+U8 = mybir.dt.uint8
+FP8X4 = mybir.dt.float8_e4m3fn_x4
+ALU = mybir.AluOpType
+ACT = mybir.ActivationFunctionType
+AXIS = mybir.AxisListType
+
+P = 128
+BATCH = 32
+TOKENS = 32
+H = 1024
+
+K_PASS = 4 * P
+PASSES = H // K_PASS
+CHUNKS = H // (2 * P)
+N_HALF = 512
+HALVES = H // N_HALF
+BLOCKS = H // P
+BLOCKS_PER_HALF = N_HALF // P
+
+BATCHES_PER_TILE = 8
+ROWS_PER_BATCH = P // BATCHES_PER_TILE
+TILES_PER_GROUP = TOKENS // ROWS_PER_BATCH
+GROUPS = BATCH // BATCHES_PER_TILE
+
+BLOCKS_BEFORE_FIRST_BANK = 1 + BLOCKS_PER_HALF + 1
+BLOCKS_PER_BANK = 2
+
+FLOPS = 2 * BATCH * TOKENS * H * H
+
+
+def tile_dynamicroutingfusion_pa_kernel(tc, text_feat, vision_proj, Wt, bt, out_0, out_1):
+    nc = tc.nc
+
+    x_dram = text_feat.flatten_outer_dims().rearrange("(g p t) k -> g t p k", p=P, t=TILES_PER_GROUP)
+    proj_dram = out_0.flatten_outer_dims().rearrange("(g p t) h -> g t p h", p=P, t=TILES_PER_GROUP)
+    weighted_dram = out_1.flatten_outer_dims().rearrange("(g p t) h -> g t p h", p=P, t=TILES_PER_GROUP)
+    w_dram = Wt.rearrange("(j p) k -> j p k", p=P)
+
+    with ExitStack() as ctx:
+        keep = ctx.enter_context(tc.tile_pool(name="keep", bufs=1))
+        stage = ctx.enter_context(tc.tile_pool(name="stage", bufs=4))
+        results = ctx.enter_context(tc.tile_pool(name="results", bufs=2 * TILES_PER_GROUP))
+        small = ctx.enter_context(tc.tile_pool(name="small", bufs=2))
+        psum_t = ctx.enter_context(tc.psum_pool(name="psum_t", bufs=3))
+        psum_acc = ctx.enter_context(tc.psum_pool(name="psum_acc", bufs=4))
+        psum_s = ctx.enter_context(tc.psum_pool(name="psum_s", bufs=1))
+
+        raw = {"x": keep.tile([P, BLOCKS, H], BF16, name="x_raw"), "w": keep.tile([P, BLOCKS, H], BF16, name="w_raw")}
+        dram = {
+            "x": [x_dram[g, t] for g in range(GROUPS) for t in range(TILES_PER_GROUP)],
+            "w": [w_dram[j] for j in range(BLOCKS)],
+        }
+        codes = {
+            "x": keep.tile([P, PASSES, H], U32, name="x_codes", align_bytes=64),
+            "w": keep.tile([P, PASSES, H], U32, name="w_codes", align_bytes=64),
+        }
+        scales = {
+            "x": keep.tile([P, PASSES, H], U8, name="x_scales", align_bytes=64),
+            "w": keep.tile([P, PASSES, H], U8, name="w_scales", align_bytes=64),
+        }
+        vision_rows = keep.tile([P, GROUPS, H], BF16)
+        bias_seed = keep.tile([P, H], BF16)
+        bias_rows = keep.tile([P, H], BF16)
+
+        def load(operand, block):
+            nc.sync.dma_start(out=raw[operand][:, block, :], in_=dram[operand][block])
+
+        def load_vision(g):
+            rows = vision_proj[g * BATCHES_PER_TILE : (g + 1) * BATCHES_PER_TILE, :, :]
+            nc.sync.dma_start(
+                out=vision_rows[:, g, :], in_=rows.to_broadcast([BATCHES_PER_TILE, ROWS_PER_BATCH, H])
+            )
+
+        in_order = [("x", 0)]
+        in_order += [("w", j) for j in range(BLOCKS_PER_HALF)]
+        in_order += [("x", t) for t in range(1, TILES_PER_GROUP)]
+        in_order += [("w", j) for j in range(BLOCKS_PER_HALF, BLOCKS)]
+        in_order += [("x", n) for n in range(TILES_PER_GROUP, BLOCKS)]
+        for operand, block in in_order:
+            load(operand, block)
+            if (operand, block) == ("w", BLOCKS_PER_HALF - 1):
+                load_vision(0)
+            if operand == "x" and block >= TILES_PER_GROUP and block % TILES_PER_GROUP == 0:
+                load_vision(block // TILES_PER_GROUP)
+
+        nc.vector.memset(bias_seed[:], 0.0)
+        nc.scalar.dma_start(out=bias_seed[0:1, :], in_=bt.unsqueeze(0))
+        ident = keep.tile([P, P], F32)
+        make_identity(nc, ident[:])
+        ones = keep.tile([P, P], BF16)
+        nc.vector.memset(ones[:], 1.0)
+        warm = keep.tile([P, 1], F32)
+        nc.vector.memset(warm[:], 0.0)
+        nc.scalar.activation(out=warm[:], in_=warm[:], func=ACT.Exp)
+        batch_of = keep.tile([P, BATCHES_PER_TILE], F32)
+        nc.vector.tensor_reduce(
+            out=batch_of[:], in_=ident[:].rearrange("p (b j) -> p b j", j=ROWS_PER_BATCH), axis=AXIS.X, op=ALU.add
+        )
+        same_batch = keep.tile([P, P], F32)
+        nc.vector.tensor_copy(
+            out=same_batch[:].rearrange("p (b j) -> p b j", j=ROWS_PER_BATCH),
+            in_=batch_of[:].unsqueeze(2).to_broadcast([P, BATCHES_PER_TILE, ROWS_PER_BATCH]),
+        )
+        place_of = keep.tile([P, ROWS_PER_BATCH], F32)
+        nc.vector.tensor_reduce(
+            out=place_of[:], in_=ident[:].rearrange("p (b j) -> p j b", j=ROWS_PER_BATCH), axis=AXIS.X, op=ALU.add
+        )
+
+        def prepare(position):
+            operand, block = in_order[position]
+            words = raw[operand][:, block, :].bitcast(F32)
+            bank = psum_t.tile([P, CHUNKS, P], F32, tag="bank")
+            for c in range(CHUNKS):
+                first_word = c // 2 * 2 * P + c % 2
+                nc.tensor.transpose(bank[:, c, :], words[:, first_word : (c // 2 + 1) * 2 * P : 2], ident[:])
+            grouped = stage.tile([P, PASSES * P * 4], BF16, align_bytes=64, tag="grouped")
+            grouped_words = grouped[:].bitcast(F32).rearrange("p (g r u) -> p g r u", g=PASSES, u=2)
+            transposed = bank[:].rearrange("p (g u) r -> p g r u", u=2)
+            if position < BLOCKS_BEFORE_FIRST_BANK and position % 2 == 1:
+                nc.vector.tensor_copy(out=grouped_words, in_=transposed)
+            else:
+                nc.scalar.copy(out=grouped_words, in_=transposed)
+            return grouped
+
+        def quantise(position, grouped):
+            operand, block = in_order[position]
+            for c in range(PASSES):
+                nc.vector.quantize_mx(
+                    out=codes[operand][:, c, block * P : (block + 1) * P].bitcast(FP8X4),
+                    scales=scales[operand][:, c, block * P : (block + 1) * P],
+                    in_=grouped[:, c * P * 4 : (c + 1) * P * 4],
+                )
+
+        def positions_from(first):
+            return range(first, min(first + BLOCKS_PER_BANK, len(in_order)))
+
+        def multiply(g, half, t):
+            block = g * TILES_PER_GROUP + t
+            acc = psum_acc.tile([P, N_HALF], F32)
+            for c in range(PASSES):
+                nc.tensor.matmul_mx(
+                    out=acc[:],
+                    lhsT=codes["x"][:, c, block * P : (block + 1) * P].bitcast(FP8X4),
+                    lhsT_scale=scales["x"][:, c, block * P : (block + 1) * P],
+                    rhs=codes["w"][:, c, half * N_HALF : (half + 1) * N_HALF].bitcast(FP8X4),
+                    rhs_scale=scales["w"][:, c, half * N_HALF : (half + 1) * N_HALF],
+                    start=(c == 0),
+                    stop=(c == PASSES - 1),
+                )
+            return acc
+
+        def finish(g, half, t, acc, coupling_parts, proj):
+            cols = slice(half * N_HALF, (half + 1) * N_HALF)
+            product = stage.tile([P, N_HALF], F32, tag="product")
+            nc.vector.scalar_tensor_tensor(
+                out=product[:],
+                in0=acc[:],
+                scalar=2.0,
+                in1=vision_rows[:, g, cols],
+                op0=ALU.mult,
+                op1=ALU.mult,
+                accum_out=coupling_parts[:, half, t : t + 1],
+            )
+            if half == 0:
+                nc.vector.tensor_tensor(out=proj[:, cols], in0=acc[:], in1=bias_rows[:, cols], op=ALU.add)
+            else:
+                bare = stage.tile([P, N_HALF], F32, tag="bare")
+                nc.scalar.copy(out=bare[:], in_=acc[:])
+                nc.gpsimd.tensor_tensor(out=proj[:, cols], in0=bare[:], in1=bias_rows[:, cols], op=ALU.add)
+            if half == HALVES - 1:
+                nc.sync.dma_start(out=proj_dram[g, t], in_=proj[:])
+
+        def spread_couplings(coupling_parts):
+            coupling = small.tile([P, TILES_PER_GROUP], F32, tag="coupling")
+            nc.vector.tensor_tensor(out=coupling[:], in0=coupling_parts[:, 0, :], in1=coupling_parts[:, 1, :], op=ALU.add)
+            spread = small.tile([P, TILES_PER_GROUP, ROWS_PER_BATCH], F32, tag="spread")
+            nc.vector.tensor_tensor(
+                out=spread[:],
+                in0=coupling[:].unsqueeze(2).to_broadcast([P, TILES_PER_GROUP, ROWS_PER_BATCH]),
+                in1=place_of[:].unsqueeze(1).to_broadcast([P, TILES_PER_GROUP, ROWS_PER_BATCH]),
+                op=ALU.mult,
+            )
+            return {"coupling": coupling, "spread": spread}
+
+        def gather_couplings(state):
+            batch_couplings = psum_s.tile([P, TOKENS], F32)
+            nc.tensor.matmul(
+                out=batch_couplings[:],
+                lhsT=same_batch[:],
+                rhs=state["spread"][:].rearrange("p t j -> p (t j)"),
+                start=True,
+                stop=True,
+            )
+            state["batch_couplings"] = batch_couplings
+
+        def exponentials(state):
+            minus_max = small.tile([P, 1], F32, tag="minus_max")
+            nc.vector.tensor_reduce(
+                out=minus_max[:], in_=state["batch_couplings"][:], axis=AXIS.X, op=ALU.max, negate=True
+            )
+            exp_all = small.tile([P, TOKENS], F32, tag="exp_all")
+            exp_sum = small.tile([P, 1], F32, tag="exp_sum")
+            nc.scalar.activation(
+                out=exp_all[:],
+                in_=state["batch_couplings"][:],
+                func=ACT.Exp,
+                bias=minus_max[:],
+                scale=1.0,
+                accum_out=exp_sum[:],
+            )
+            exp_own = small.tile([P, TILES_PER_GROUP], F32, tag="exp_own")
+            nc.scalar.activation(out=exp_own[:], in_=state["coupling"][:], func=ACT.Exp, bias=minus_max[:], scale=1.0)
+            state["exp_sum"] = exp_sum
+            state["exp_own"] = exp_own
+
+        def normalise(state):
+            inverse_sum = small.tile([P, 1], F32, tag="inverse_sum")
+            nc.vector.reciprocal(out=inverse_sum[:], in_=state["exp_sum"][:])
+            routing = small.tile([P, TILES_PER_GROUP], F32, tag="routing")
+            nc.vector.tensor_scalar(
+                out=routing[:], in0=state["exp_own"][:], scalar1=inverse_sum[:, 0:1], scalar2=None, op0=ALU.mult
+            )
+            state["routing"] = routing
+
+        def weigh(g, t, state):
+            weight = state["routing"][:, t : t + 1]
+            weighted = results.tile([P, H], F32, tag="weighted")
+            nc.scalar.activation(out=weighted[:, 0:N_HALF], in_=vision_rows[:, g, 0:N_HALF], func=ACT.Copy, scale=weight)
+            nc.gpsimd.tensor_scalar(
+                out=weighted[:, N_HALF:H],
+                in0=vision_rows[:, g, N_HALF:H],
+                scalar1=weight,
+                scalar2=0.0,
+                op0=ALU.mult,
+                op1=ALU.add,
+            )
+            nc.sync.dma_start(out=weighted_dram[g, t], in_=weighted[:])
+
+        banks = [(0, half, t) for half in range(HALVES) for t in range(TILES_PER_GROUP)]
+        banks += [(g, half, t) for g in range(1, GROUPS) for t in range(TILES_PER_GROUP) for half in range(HALVES)]
+        coupling_parts = [small.tile([P, HALVES, TILES_PER_GROUP], F32, name="coupling_parts") for g in range(GROUPS)]
+
+        for first in range(0, BLOCKS_BEFORE_FIRST_BANK, BLOCKS_PER_BANK):
+            grouped_tiles = [prepare(position) for position in positions_from(first)]
+            for position, grouped in zip(positions_from(first), grouped_tiles):
+                quantise(position, grouped)
+        bias_bank = psum_t.tile([P, H], BF16, tag="bank")
+        for half in range(HALVES):
+            cols = slice(half * N_HALF, (half + 1) * N_HALF)
+            nc.tensor.matmul(out=bias_bank[:, cols], lhsT=ones[:], rhs=bias_seed[:, cols], start=True, stop=True)
+        nc.scalar.copy(out=bias_rows[:], in_=bias_bank[:])
+        acc = multiply(0, 0, 0)
+
+        state = None
+        proj_tiles = None
+        for i in range(len(banks)):
+            g, half, t = banks[i]
+            bank_number = i % (HALVES * TILES_PER_GROUP)
+            if bank_number == 0:
+                proj_tiles = [results.tile([P, H], F32, name="proj", tag="proj") for n in range(TILES_PER_GROUP)]
+            first = BLOCKS_BEFORE_FIRST_BANK + i * BLOCKS_PER_BANK
+            grouped_tiles = [prepare(position) for position in positions_from(first)]
+            finish(g, half, t, acc, coupling_parts[g], proj_tiles[t])
+            for position, grouped in zip(positions_from(first), grouped_tiles):
+                quantise(position, grouped)
+            if i + 1 < len(banks):
+                acc = multiply(banks[i + 1][0], banks[i + 1][1], banks[i + 1][2])
+            if g > 0 and bank_number == 0:
+                gather_couplings(state)
+                exponentials(state)
+            if g > 0 and bank_number == 1:
+                normalise(state)
+            if g > 0 and 2 <= bank_number < 2 + TILES_PER_GROUP:
+                weigh(g - 1, bank_number - 2, state)
+            if bank_number == HALVES * TILES_PER_GROUP - 1:
+                state = spread_couplings(coupling_parts[g])
+        gather_couplings(state)
+        exponentials(state)
+        normalise(state)
+        for t in range(TILES_PER_GROUP):
+            weigh(GROUPS - 1, t, state)

@@ -67,17 +67,11 @@ def tile_dynamicroutingfusion_pa_kernel(tc, text_feat, vision_proj, Wt, bt, out_
             "w": keep.tile([P, PASSES, H], U8, name="w_scales", align_bytes=64),
         }
         vision_rows = keep.tile([P, GROUPS, H], BF16)
-        bias_seed = keep.tile([P, H], BF16)
+        seed = keep.tile([P, H], BF16)
         bias_rows = keep.tile([P, H], BF16)
 
         def load(operand, block):
             nc.sync.dma_start(out=raw[operand][:, block, :], in_=dram[operand][block])
-
-        def load_vision(g):
-            rows = vision_proj[g * BATCHES_PER_TILE : (g + 1) * BATCHES_PER_TILE, :, :]
-            nc.sync.dma_start(
-                out=vision_rows[:, g, :], in_=rows.to_broadcast([BATCHES_PER_TILE, ROWS_PER_BATCH, H])
-            )
 
         in_order = [("x", 0)]
         in_order += [("w", j) for j in range(BLOCKS_PER_HALF)]
@@ -86,17 +80,20 @@ def tile_dynamicroutingfusion_pa_kernel(tc, text_feat, vision_proj, Wt, bt, out_
         in_order += [("x", n) for n in range(TILES_PER_GROUP, BLOCKS)]
         for operand, block in in_order:
             load(operand, block)
-            if (operand, block) == ("w", BLOCKS_PER_HALF - 1):
-                load_vision(0)
-            if operand == "x" and block >= TILES_PER_GROUP and block % TILES_PER_GROUP == 0:
-                load_vision(block // TILES_PER_GROUP)
 
-        nc.vector.memset(bias_seed[:], 0.0)
-        nc.scalar.dma_start(out=bias_seed[0:1, :], in_=bt.unsqueeze(0))
+        nc.vector.memset(seed[:].bitcast(F32), 0.0)
+        nc.scalar.dma_start(out=seed[0:BATCH, :], in_=vision_proj.flatten_outer_dims())
+        nc.scalar.dma_start(out=seed[BATCH : BATCH + 1, :], in_=bt.unsqueeze(0))
         ident = keep.tile([P, P], F32)
         make_identity(nc, ident[:])
-        ones = keep.tile([P, P], BF16)
-        nc.vector.memset(ones[:], 1.0)
+        pick_rows = keep.tile([P, BATCH + BATCHES_PER_TILE, ROWS_PER_BATCH], BF16)
+        nc.vector.tensor_copy(
+            out=pick_rows[:, 0:BATCH, :], in_=ident[:, 0:BATCH].unsqueeze(2).to_broadcast([P, BATCH, ROWS_PER_BATCH])
+        )
+        nc.vector.tensor_copy(
+            out=pick_rows[:, BATCH : BATCH + BATCHES_PER_TILE, :],
+            in_=ident[:, BATCH : BATCH + 1].unsqueeze(2).to_broadcast([P, BATCHES_PER_TILE, ROWS_PER_BATCH]),
+        )
         warm = keep.tile([P, 1], F32)
         nc.vector.memset(warm[:], 0.0)
         nc.scalar.activation(out=warm[:], in_=warm[:], func=ACT.Exp)
@@ -141,6 +138,14 @@ def tile_dynamicroutingfusion_pa_kernel(tc, text_feat, vision_proj, Wt, bt, out_
 
         def positions_from(first):
             return range(first, min(first + BLOCKS_PER_BANK, len(in_order)))
+
+        def spread_rows(out, first):
+            bank = psum_t.tile([P, H], BF16, tag="bank")
+            lhsT = pick_rows[:, first : first + BATCHES_PER_TILE, :].rearrange("p b j -> p (b j)")
+            for half in range(HALVES):
+                cols = slice(half * N_HALF, (half + 1) * N_HALF)
+                nc.tensor.matmul(out=bank[:, cols], lhsT=lhsT, rhs=seed[:, cols], start=True, stop=True)
+            nc.scalar.copy(out=out, in_=bank[:])
 
         def multiply(g, half, t):
             block = g * TILES_PER_GROUP + t
@@ -252,11 +257,8 @@ def tile_dynamicroutingfusion_pa_kernel(tc, text_feat, vision_proj, Wt, bt, out_
             grouped_tiles = [prepare(position) for position in positions_from(first)]
             for position, grouped in zip(positions_from(first), grouped_tiles):
                 quantise(position, grouped)
-        bias_bank = psum_t.tile([P, H], BF16, tag="bank")
-        for half in range(HALVES):
-            cols = slice(half * N_HALF, (half + 1) * N_HALF)
-            nc.tensor.matmul(out=bias_bank[:, cols], lhsT=ones[:], rhs=bias_seed[:, cols], start=True, stop=True)
-        nc.scalar.copy(out=bias_rows[:], in_=bias_bank[:])
+        spread_rows(vision_rows[:, 0, :], 0)
+        spread_rows(bias_rows[:], BATCH)
         acc = multiply(0, 0, 0)
 
         state = None
@@ -273,6 +275,8 @@ def tile_dynamicroutingfusion_pa_kernel(tc, text_feat, vision_proj, Wt, bt, out_
                 quantise(position, grouped)
             if i + 1 < len(banks):
                 acc = multiply(banks[i + 1][0], banks[i + 1][1], banks[i + 1][2])
+            if bank_number == 1 and g + 1 < GROUPS:
+                spread_rows(vision_rows[:, g + 1, :], (g + 1) * BATCHES_PER_TILE)
             if g > 0 and bank_number == 0:
                 gather_couplings(state)
                 exponentials(state)

@@ -19,19 +19,19 @@ H = 1024
 
 K_PASS = 4 * P
 PASSES = H // K_PASS
-CHUNKS = H // (2 * P)
+WORDS = K_PASS // 2
 N_HALF = 512
 HALVES = H // N_HALF
-BLOCKS = H // P
-BLOCKS_PER_HALF = N_HALF // P
 
-BATCHES_PER_TILE = 8
-ROWS_PER_BATCH = P // BATCHES_PER_TILE
-TILES_PER_GROUP = TOKENS // ROWS_PER_BATCH
-GROUPS = BATCH // BATCHES_PER_TILE
-
-BLOCKS_BEFORE_FIRST_BANK = 1 + BLOCKS_PER_HALF + 1
-BLOCKS_PER_BANK = 2
+ROWS = 2
+UNIT = ROWS * P
+V_PART = 384
+VS_PART = 1024
+V_BIAS = ((0, 1, 0), (0, 1, 1), (1, 1, 0), (1, 1, 1), (2, 1, 0), (3, 1, 0), (3, 1, 1))
+QUARTERS = P // BATCH
+UNITS = H // UNIT
+BATCHES = UNIT // TOKENS
+SHARE = P // BATCHES
 
 FLOPS = 2 * BATCH * TOKENS * H * H
 
@@ -39,24 +39,22 @@ FLOPS = 2 * BATCH * TOKENS * H * H
 def tile_dynamicroutingfusion_pa_kernel(tc, text_feat, vision_proj, Wt, bt, out_0, out_1):
     nc = tc.nc
 
-    x_dram = text_feat.flatten_outer_dims().rearrange("(g p t) k -> g t p k", p=P, t=TILES_PER_GROUP)
-    proj_dram = out_0.flatten_outer_dims().rearrange("(g p t) h -> g t p h", p=P, t=TILES_PER_GROUP)
-    weighted_dram = out_1.flatten_outer_dims().rearrange("(g p t) h -> g t p h", p=P, t=TILES_PER_GROUP)
-    w_dram = Wt.rearrange("(j p) k -> j p k", p=P)
+    x_dram = text_feat.flatten_outer_dims().rearrange("(g p t) k -> g p t k", p=P, t=ROWS)
+    w_dram = Wt.rearrange("(g p t) k -> g p t k", p=P, t=ROWS)
+    proj_dram = out_0.flatten_outer_dims().rearrange("(g p t) h -> g t p h", p=P, t=ROWS)
+    weighted_dram = out_1.flatten_outer_dims().rearrange("(g p t) h -> g t p h", p=P, t=ROWS)
 
     with ExitStack() as ctx:
         keep = ctx.enter_context(tc.tile_pool(name="keep", bufs=1))
         stage = ctx.enter_context(tc.tile_pool(name="stage", bufs=4))
-        results = ctx.enter_context(tc.tile_pool(name="results", bufs=2 * TILES_PER_GROUP))
+        results = ctx.enter_context(tc.tile_pool(name="results", bufs=2 * ROWS))
         small = ctx.enter_context(tc.tile_pool(name="small", bufs=2))
-        psum_t = ctx.enter_context(tc.psum_pool(name="psum_t", bufs=3))
+        psum_t = ctx.enter_context(tc.psum_pool(name="psum_t", bufs=4))
         psum_acc = ctx.enter_context(tc.psum_pool(name="psum_acc", bufs=4))
-        psum_s = ctx.enter_context(tc.psum_pool(name="psum_s", bufs=1))
 
-        raw = {"x": keep.tile([P, BLOCKS, H], BF16, name="x_raw"), "w": keep.tile([P, BLOCKS, H], BF16, name="w_raw")}
-        dram = {
-            "x": [x_dram[g, t] for g in range(GROUPS) for t in range(TILES_PER_GROUP)],
-            "w": [w_dram[j] for j in range(BLOCKS)],
+        raw = {
+            "x": keep.tile([P, UNITS, ROWS, H], BF16, name="x_raw"),
+            "w": keep.tile([P, UNITS, ROWS, H], BF16, name="w_raw"),
         }
         codes = {
             "x": keep.tile([P, PASSES, H], U32, name="x_codes", align_bytes=64),
@@ -66,95 +64,106 @@ def tile_dynamicroutingfusion_pa_kernel(tc, text_feat, vision_proj, Wt, bt, out_
             "x": keep.tile([P, PASSES, H], U8, name="x_scales", align_bytes=64),
             "w": keep.tile([P, PASSES, H], U8, name="w_scales", align_bytes=64),
         }
-        vision_rows = keep.tile([P, GROUPS, H], BF16)
-        seed = keep.tile([P, H], BF16)
+        vision_rows = keep.tile([P, UNITS, H], BF16)
+        vision_seed = keep.tile([P, H // QUARTERS], BF16)
+        bias_seed = keep.tile([P, H], BF16)
         bias_rows = keep.tile([P, H], BF16)
 
-        def load(operand, block):
-            nc.sync.dma_start(out=raw[operand][:, block, :], in_=dram[operand][block])
+        nc.vector.memset(bias_seed[:].bitcast(F32), 0.0)
+        nc.sync.dma_start(
+            out=vision_seed[:], in_=vision_proj.flatten_outer_dims().rearrange("b (q h) -> (b q) h", q=QUARTERS)
+        )
+        nc.sync.dma_start(out=bias_seed[0:1, :], in_=bt.unsqueeze(0))
+        order = [("x", 0)] + [("w", u) for u in range(UNITS)] + [("x", u) for u in range(1, UNITS)]
+        dram = {"x": x_dram, "w": w_dram}
+        for operand, unit in order:
+            nc.sync.dma_start(out=raw[operand][:, unit, :, :], in_=dram[operand][unit])
 
-        in_order = [("x", 0)]
-        in_order += [("w", j) for j in range(BLOCKS_PER_HALF)]
-        in_order += [("x", t) for t in range(1, TILES_PER_GROUP)]
-        in_order += [("w", j) for j in range(BLOCKS_PER_HALF, BLOCKS)]
-        in_order += [("x", n) for n in range(TILES_PER_GROUP, BLOCKS)]
-        for operand, block in in_order:
-            load(operand, block)
-
-        nc.vector.memset(seed[:].bitcast(F32), 0.0)
-        nc.scalar.dma_start(out=seed[0:BATCH, :], in_=vision_proj.flatten_outer_dims())
-        nc.scalar.dma_start(out=seed[BATCH : BATCH + 1, :], in_=bt.unsqueeze(0))
         ident = keep.tile([P, P], F32)
         make_identity(nc, ident[:])
-        pick_rows = keep.tile([P, BATCH + BATCHES_PER_TILE, ROWS_PER_BATCH], BF16)
-        nc.vector.tensor_copy(
-            out=pick_rows[:, 0:BATCH, :], in_=ident[:, 0:BATCH].unsqueeze(2).to_broadcast([P, BATCH, ROWS_PER_BATCH])
-        )
-        nc.vector.tensor_copy(
-            out=pick_rows[:, BATCH : BATCH + BATCHES_PER_TILE, :],
-            in_=ident[:, BATCH : BATCH + 1].unsqueeze(2).to_broadcast([P, BATCHES_PER_TILE, ROWS_PER_BATCH]),
-        )
+        pick = keep.tile([P, QUARTERS, BATCH, SHARE], BF16)
+        for first, end in ((0, BATCHES), (BATCHES, BATCH)):
+            nc.vector.tensor_copy(
+                out=pick[:, :, first:end, :],
+                in_=ident[:]
+                .rearrange("p (b q) -> p q b", q=QUARTERS)[:, :, first:end]
+                .unsqueeze(3)
+                .to_broadcast([P, QUARTERS, end - first, SHARE]),
+            )
+        ones = keep.tile([P, P], BF16)
+        nc.vector.memset(ones[:], 1.0)
         warm = keep.tile([P, 1], F32)
         nc.vector.memset(warm[:], 0.0)
         nc.scalar.activation(out=warm[:], in_=warm[:], func=ACT.Exp)
-        batch_of = keep.tile([P, BATCHES_PER_TILE], F32)
+        batch_of = keep.tile([P, BATCHES], F32)
         nc.vector.tensor_reduce(
-            out=batch_of[:], in_=ident[:].rearrange("p (b j) -> p b j", j=ROWS_PER_BATCH), axis=AXIS.X, op=ALU.add
+            out=batch_of[:], in_=ident[:].rearrange("p (b j) -> p b j", j=SHARE), axis=AXIS.X, op=ALU.add
         )
         same_batch = keep.tile([P, P], F32)
         nc.vector.tensor_copy(
-            out=same_batch[:].rearrange("p (b j) -> p b j", j=ROWS_PER_BATCH),
-            in_=batch_of[:].unsqueeze(2).to_broadcast([P, BATCHES_PER_TILE, ROWS_PER_BATCH]),
+            out=same_batch[:].rearrange("p (b j) -> p b j", j=SHARE),
+            in_=batch_of[:].unsqueeze(2).to_broadcast([P, BATCHES, SHARE]),
         )
-        place_of = keep.tile([P, ROWS_PER_BATCH], F32)
+        place_of = keep.tile([P, SHARE], F32)
         nc.vector.tensor_reduce(
-            out=place_of[:], in_=ident[:].rearrange("p (b j) -> p j b", j=ROWS_PER_BATCH), axis=AXIS.X, op=ALU.add
+            out=place_of[:], in_=ident[:].rearrange("p (b j) -> p j b", j=SHARE), axis=AXIS.X, op=ALU.add
         )
 
-        def prepare(position):
-            operand, block = in_order[position]
-            words = raw[operand][:, block, :].bitcast(F32)
-            bank = psum_t.tile([P, CHUNKS, P], F32, tag="bank")
-            for c in range(CHUNKS):
-                first_word = c // 2 * 2 * P + c % 2
-                nc.tensor.transpose(bank[:, c, :], words[:, first_word : (c // 2 + 1) * 2 * P : 2], ident[:])
-            grouped = stage.tile([P, PASSES * P * 4], BF16, align_bytes=64, tag="grouped")
-            grouped_words = grouped[:].bitcast(F32).rearrange("p (g r u) -> p g r u", g=PASSES, u=2)
-            transposed = bank[:].rearrange("p (g u) r -> p g r u", u=2)
-            if position < BLOCKS_BEFORE_FIRST_BANK and position % 2 == 1:
-                nc.vector.tensor_copy(out=grouped_words, in_=transposed)
+        steps = [(operand, unit, c) for operand, unit in order for c in range(PASSES)]
+
+        def transpose(step):
+            operand, unit, c = steps[step]
+            bank = psum_t.tile([P, 2, ROWS, P], F32, tag="bank")
+            for t in range(ROWS):
+                words = raw[operand][:, unit, t, :].bitcast(F32)
+                for u in range(2):
+                    nc.tensor.transpose(bank[:, u, t, :], words[:, c * WORDS + u : (c + 1) * WORDS : 2], ident[:])
+            return bank
+
+        def regroup(step, bank, copy):
+            operand, unit, c = steps[step]
+            grouped = stage.tile([P, UNIT * 4], BF16, align_bytes=64, tag="grouped")
+            if operand == "x":
+                out = grouped[:].bitcast(F32).rearrange("p (t r u) -> p t r u", t=ROWS, u=2)
+                in_ = bank[:].rearrange("p u t r -> p t r u")
             else:
-                nc.scalar.copy(out=grouped_words, in_=transposed)
+                out = grouped[:].bitcast(F32).rearrange("p (r t u) -> p r t u", t=ROWS, u=2)
+                in_ = bank[:].rearrange("p u t r -> p r t u")
+            copy(out=out, in_=in_)
             return grouped
 
-        def quantise(position, grouped):
-            operand, block = in_order[position]
-            for c in range(PASSES):
-                nc.vector.quantize_mx(
-                    out=codes[operand][:, c, block * P : (block + 1) * P].bitcast(FP8X4),
-                    scales=scales[operand][:, c, block * P : (block + 1) * P],
-                    in_=grouped[:, c * P * 4 : (c + 1) * P * 4],
-                )
+        def quantise(step, grouped):
+            operand, unit, c = steps[step]
+            nc.vector.quantize_mx(
+                out=codes[operand][:, c, unit * UNIT : (unit + 1) * UNIT].bitcast(FP8X4),
+                scales=scales[operand][:, c, unit * UNIT : (unit + 1) * UNIT],
+                in_=grouped[:],
+            )
 
-        def positions_from(first):
-            return range(first, min(first + BLOCKS_PER_BANK, len(in_order)))
-
-        def spread_rows(out, first):
+        def spread_vision(g):
             bank = psum_t.tile([P, H], BF16, tag="bank")
-            lhsT = pick_rows[:, first : first + BATCHES_PER_TILE, :].rearrange("p b j -> p (b j)")
+            width = H // QUARTERS
+            for q in range(QUARTERS):
+                lhsT = pick[:, q, g * BATCHES : (g + 1) * BATCHES, :].rearrange("p b j -> p (b j)")
+                cols = slice(q * width, (q + 1) * width)
+                nc.tensor.matmul(out=bank[:, cols], lhsT=lhsT, rhs=vision_seed[:], start=True, stop=True)
+            return bank
+
+        def spread_bias():
+            bank = psum_t.tile([P, H], BF16, tag="bank")
             for half in range(HALVES):
                 cols = slice(half * N_HALF, (half + 1) * N_HALF)
-                nc.tensor.matmul(out=bank[:, cols], lhsT=lhsT, rhs=seed[:, cols], start=True, stop=True)
-            nc.scalar.copy(out=out, in_=bank[:])
+                nc.tensor.matmul(out=bank[:, cols], lhsT=ones[:], rhs=bias_seed[:, cols], start=True, stop=True)
+            return bank
 
         def multiply(g, half, t):
-            block = g * TILES_PER_GROUP + t
+            first = g * UNIT + t * P
             acc = psum_acc.tile([P, N_HALF], F32)
             for c in range(PASSES):
                 nc.tensor.matmul_mx(
                     out=acc[:],
-                    lhsT=codes["x"][:, c, block * P : (block + 1) * P].bitcast(FP8X4),
-                    lhsT_scale=scales["x"][:, c, block * P : (block + 1) * P],
+                    lhsT=codes["x"][:, c, first : first + P].bitcast(FP8X4),
+                    lhsT_scale=scales["x"][:, c, first : first + P],
                     rhs=codes["w"][:, c, half * N_HALF : (half + 1) * N_HALF].bitcast(FP8X4),
                     rhs_scale=scales["w"][:, c, half * N_HALF : (half + 1) * N_HALF],
                     start=(c == 0),
@@ -162,7 +171,7 @@ def tile_dynamicroutingfusion_pa_kernel(tc, text_feat, vision_proj, Wt, bt, out_
                 )
             return acc
 
-        def finish(g, half, t, acc, coupling_parts, proj):
+        def agree(g, half, t, acc, coupling_parts):
             cols = slice(half * N_HALF, (half + 1) * N_HALF)
             product = stage.tile([P, N_HALF], F32, tag="product")
             nc.vector.scalar_tensor_tensor(
@@ -174,7 +183,10 @@ def tile_dynamicroutingfusion_pa_kernel(tc, text_feat, vision_proj, Wt, bt, out_
                 op1=ALU.mult,
                 accum_out=coupling_parts[:, half, t : t + 1],
             )
-            if half == 0:
+
+        def add_bias(g, half, t, acc, proj, by_vector):
+            cols = slice(half * N_HALF, (half + 1) * N_HALF)
+            if by_vector:
                 nc.vector.tensor_tensor(out=proj[:, cols], in0=acc[:], in1=bias_rows[:, cols], op=ALU.add)
             else:
                 bare = stage.tile([P, N_HALF], F32, tag="bare")
@@ -184,19 +196,19 @@ def tile_dynamicroutingfusion_pa_kernel(tc, text_feat, vision_proj, Wt, bt, out_
                 nc.sync.dma_start(out=proj_dram[g, t], in_=proj[:])
 
         def spread_couplings(coupling_parts):
-            coupling = small.tile([P, TILES_PER_GROUP], F32, tag="coupling")
+            coupling = small.tile([P, ROWS], F32, tag="coupling")
             nc.vector.tensor_tensor(out=coupling[:], in0=coupling_parts[:, 0, :], in1=coupling_parts[:, 1, :], op=ALU.add)
-            spread = small.tile([P, TILES_PER_GROUP, ROWS_PER_BATCH], F32, tag="spread")
+            spread = small.tile([P, ROWS, SHARE], F32, tag="spread")
             nc.vector.tensor_tensor(
                 out=spread[:],
-                in0=coupling[:].unsqueeze(2).to_broadcast([P, TILES_PER_GROUP, ROWS_PER_BATCH]),
-                in1=place_of[:].unsqueeze(1).to_broadcast([P, TILES_PER_GROUP, ROWS_PER_BATCH]),
+                in0=coupling[:].unsqueeze(2).to_broadcast([P, ROWS, SHARE]),
+                in1=place_of[:].unsqueeze(1).to_broadcast([P, ROWS, SHARE]),
                 op=ALU.mult,
             )
             return {"coupling": coupling, "spread": spread}
 
         def gather_couplings(state):
-            batch_couplings = psum_s.tile([P, TOKENS], F32)
+            batch_couplings = psum_t.tile([P, TOKENS], F32, tag="bank")
             nc.tensor.matmul(
                 out=batch_couplings[:],
                 lhsT=same_batch[:],
@@ -221,7 +233,7 @@ def tile_dynamicroutingfusion_pa_kernel(tc, text_feat, vision_proj, Wt, bt, out_
                 scale=1.0,
                 accum_out=exp_sum[:],
             )
-            exp_own = small.tile([P, TILES_PER_GROUP], F32, tag="exp_own")
+            exp_own = small.tile([P, ROWS], F32, tag="exp_own")
             nc.scalar.activation(out=exp_own[:], in_=state["coupling"][:], func=ACT.Exp, bias=minus_max[:], scale=1.0)
             state["exp_sum"] = exp_sum
             state["exp_own"] = exp_own
@@ -229,65 +241,138 @@ def tile_dynamicroutingfusion_pa_kernel(tc, text_feat, vision_proj, Wt, bt, out_
         def normalise(state):
             inverse_sum = small.tile([P, 1], F32, tag="inverse_sum")
             nc.vector.reciprocal(out=inverse_sum[:], in_=state["exp_sum"][:])
-            routing = small.tile([P, TILES_PER_GROUP], F32, tag="routing")
-            nc.vector.tensor_scalar(
-                out=routing[:], in0=state["exp_own"][:], scalar1=inverse_sum[:, 0:1], scalar2=None, op0=ALU.mult
-            )
+            routing = small.tile([P, ROWS], F32, tag="routing")
+            nc.scalar.activation(out=routing[:], in_=state["exp_own"][:], func=ACT.Copy, scale=inverse_sum[:])
+            state["inverse_sum"] = inverse_sum
             state["routing"] = routing
 
         def weigh(g, t, state):
-            weight = state["routing"][:, t : t + 1]
             weighted = results.tile([P, H], F32, tag="weighted")
-            nc.scalar.activation(out=weighted[:, 0:N_HALF], in_=vision_rows[:, g, 0:N_HALF], func=ACT.Copy, scale=weight)
-            nc.gpsimd.tensor_scalar(
-                out=weighted[:, N_HALF:H],
-                in0=vision_rows[:, g, N_HALF:H],
-                scalar1=weight,
-                scalar2=0.0,
+            nc.vector.tensor_scalar(
+                out=weighted[:, 0:V_PART],
+                in0=vision_rows[:, g, 0:V_PART],
+                scalar1=state["exp_own"][:, t : t + 1],
+                scalar2=state["inverse_sum"][:, 0:1],
                 op0=ALU.mult,
-                op1=ALU.add,
+                op1=ALU.mult,
             )
+            nc.scalar.activation(
+                out=weighted[:, V_PART:VS_PART],
+                in_=vision_rows[:, g, V_PART:VS_PART],
+                func=ACT.Copy,
+                scale=state["routing"][:, t : t + 1],
+            )
+            if VS_PART < H:
+                nc.gpsimd.tensor_scalar(
+                    out=weighted[:, VS_PART:H],
+                    in0=vision_rows[:, g, VS_PART:H],
+                    scalar1=state["exp_own"][:, t : t + 1],
+                    scalar2=state["inverse_sum"][:, 0:1],
+                    op0=ALU.mult,
+                    op1=ALU.mult,
+                )
             nc.sync.dma_start(out=weighted_dram[g, t], in_=weighted[:])
 
-        banks = [(0, half, t) for half in range(HALVES) for t in range(TILES_PER_GROUP)]
-        banks += [(g, half, t) for g in range(1, GROUPS) for t in range(TILES_PER_GROUP) for half in range(HALVES)]
-        coupling_parts = [small.tile([P, HALVES, TILES_PER_GROUP], F32, name="coupling_parts") for g in range(GROUPS)]
+        proj_tiles = {}
+        accs = {}
+        coupling_parts = [small.tile([P, HALVES, ROWS], F32, name="coupling_parts") for g in range(UNITS)]
 
-        for first in range(0, BLOCKS_BEFORE_FIRST_BANK, BLOCKS_PER_BANK):
-            grouped_tiles = [prepare(position) for position in positions_from(first)]
-            for position, grouped in zip(positions_from(first), grouped_tiles):
-                quantise(position, grouped)
-        spread_rows(vision_rows[:, 0, :], 0)
-        spread_rows(bias_rows[:], BATCH)
-        acc = multiply(0, 0, 0)
+        def start_bank(g, half, t):
+            accs[g, half, t] = multiply(g, half, t)
 
-        state = None
-        proj_tiles = None
-        for i in range(len(banks)):
-            g, half, t = banks[i]
-            bank_number = i % (HALVES * TILES_PER_GROUP)
-            if bank_number == 0:
-                proj_tiles = [results.tile([P, H], F32, name="proj", tag="proj") for n in range(TILES_PER_GROUP)]
-            first = BLOCKS_BEFORE_FIRST_BANK + i * BLOCKS_PER_BANK
-            grouped_tiles = [prepare(position) for position in positions_from(first)]
-            finish(g, half, t, acc, coupling_parts[g], proj_tiles[t])
-            for position, grouped in zip(positions_from(first), grouped_tiles):
-                quantise(position, grouped)
-            if i + 1 < len(banks):
-                acc = multiply(banks[i + 1][0], banks[i + 1][1], banks[i + 1][2])
-            if bank_number == 1 and g + 1 < GROUPS:
-                spread_rows(vision_rows[:, g + 1, :], (g + 1) * BATCHES_PER_TILE)
-            if g > 0 and bank_number == 0:
-                gather_couplings(state)
-                exponentials(state)
-            if g > 0 and bank_number == 1:
-                normalise(state)
-            if g > 0 and 2 <= bank_number < 2 + TILES_PER_GROUP:
-                weigh(g - 1, bank_number - 2, state)
-            if bank_number == HALVES * TILES_PER_GROUP - 1:
-                state = spread_couplings(coupling_parts[g])
+        def finish_coupling(g, half, t):
+            agree(g, half, t, accs[g, half, t], coupling_parts[g])
+
+        def finish_rows(g, half, t):
+            if (g, t) not in proj_tiles:
+                proj_tiles[g, t] = results.tile([P, H], F32, name="proj", tag="proj")
+            add_bias(g, half, t, accs[g, half, t], proj_tiles[g, t], (g, half, t) in V_BIAS)
+
+        def transpose_unit(n):
+            for c in range(PASSES):
+                transposed[n, c] = transpose(n * PASSES + c)
+
+        def regroup_unit(n, copies):
+            for c in range(PASSES):
+                grouped[n, c] = regroup(n * PASSES + c, transposed[n, c], copies[c])
+
+        def quantise_unit(n):
+            for c in range(PASSES):
+                quantise(n * PASSES + c, grouped[n, c])
+
+        transposed = {}
+        grouped = {}
+        on_scalar = (nc.scalar.copy, nc.scalar.copy)
+        on_both = (nc.scalar.copy, nc.vector.tensor_copy)
+        vision_bank = spread_vision(0)
+        bias_bank = spread_bias()
+        nc.scalar.copy(out=vision_rows[:, 0, :], in_=vision_bank[:])
+        nc.scalar.copy(out=bias_rows[:], in_=bias_bank[:])
+        for n in (0, 1, 2):
+            transpose_unit(n)
+            regroup_unit(n, on_both)
+            quantise_unit(n)
+        transpose_unit(3)
+        regroup_unit(3, on_scalar)
+        transpose_unit(4)
+        quantise_unit(3)
+        start_bank(0, 0, 0)
+        start_bank(0, 0, 1)
+        regroup_unit(4, on_scalar)
+        quantise_unit(4)
+        start_bank(0, 1, 0)
+        start_bank(0, 1, 1)
+        transpose_unit(5)
+        finish_coupling(0, 0, 0)
+        regroup_unit(5, on_scalar)
+        finish_rows(0, 0, 0)
+        finish_coupling(0, 1, 0)
+        finish_rows(0, 1, 0)
+        finish_coupling(0, 0, 1)
+        quantise_unit(5)
+        start_bank(1, 0, 0)
+        finish_rows(0, 0, 1)
+        finish_coupling(0, 1, 1)
+        finish_rows(0, 1, 1)
+        vision_bank = spread_vision(1)
+        state = spread_couplings(coupling_parts[0])
+        start_bank(1, 1, 0)
+        nc.scalar.copy(out=vision_rows[:, 1, :], in_=vision_bank[:])
         gather_couplings(state)
+
+        for g in range(1, UNITS):
+            last = g == UNITS - 1
+            ahead = 1 + UNITS + g
+            if not last:
+                transpose_unit(ahead)
+                vision_bank = spread_vision(g + 1)
+            finish_coupling(g, 0, 0)
+            exponentials(state)
+            if not last:
+                regroup_unit(ahead, on_scalar)
+            finish_rows(g, 0, 0)
+            start_bank(g, 0, 1)
+            finish_coupling(g, 1, 0)
+            finish_rows(g, 1, 0)
+            normalise(state)
+            start_bank(g, 1, 1)
+            if not last:
+                quantise_unit(ahead)
+            finish_coupling(g, 0, 1)
+            weigh(g - 1, 0, state)
+            finish_rows(g, 0, 1)
+            if not last:
+                start_bank(g + 1, 0, 0)
+            finish_coupling(g, 1, 1)
+            weigh(g - 1, 1, state)
+            state = spread_couplings(coupling_parts[g])
+            if not last:
+                finish_rows(g, 1, 1)
+                start_bank(g + 1, 1, 0)
+                nc.scalar.copy(out=vision_rows[:, g + 1, :], in_=vision_bank[:])
+            gather_couplings(state)
+        finish_rows(UNITS - 1, 1, 1)
         exponentials(state)
         normalise(state)
-        for t in range(TILES_PER_GROUP):
-            weigh(GROUPS - 1, t, state)
+        for t in range(ROWS):
+            weigh(UNITS - 1, t, state)

@@ -25,9 +25,9 @@ HALVES = H // N_HALF
 
 ROWS = 2
 UNIT = ROWS * P
-V_PART = 384
-VS_PART = 1024
-V_BIAS = ((0, 1, 0), (0, 1, 1), (1, 1, 0), (1, 1, 1), (2, 1, 0), (3, 1, 0), (3, 1, 1))
+V_PART = 0
+VS_PART = 576
+V_BIAS = ((0, 1, 0), (0, 1, 1), (1, 1, 0), (1, 1, 1), (2, 1, 0), (2, 1, 1), (3, 1, 0), (3, 1, 1))
 QUARTERS = P // BATCH
 UNITS = H // UNIT
 BATCHES = UNIT // TOKENS
@@ -197,14 +197,15 @@ def tile_dynamicroutingfusion_pa_kernel(tc, text_feat, vision_proj, Wt, bt, out_
 
         def spread_couplings(coupling_parts):
             coupling = small.tile([P, ROWS], F32, tag="coupling")
-            nc.vector.tensor_tensor(out=coupling[:], in0=coupling_parts[:, 0, :], in1=coupling_parts[:, 1, :], op=ALU.add)
             spread = small.tile([P, ROWS, SHARE], F32, tag="spread")
-            nc.vector.tensor_tensor(
-                out=spread[:],
-                in0=coupling[:].unsqueeze(2).to_broadcast([P, ROWS, SHARE]),
-                in1=place_of[:].unsqueeze(1).to_broadcast([P, ROWS, SHARE]),
-                op=ALU.mult,
-            )
+            for t in range(ROWS):
+                nc.scalar.activation(
+                    out=coupling[:, t : t + 1],
+                    in_=coupling_parts[:, 0, t : t + 1],
+                    func=ACT.Identity,
+                    bias=coupling_parts[:, 1, t : t + 1],
+                )
+                nc.scalar.activation(out=spread[:, t, :], in_=place_of[:], func=ACT.Copy, scale=coupling[:, t : t + 1])
             return {"coupling": coupling, "spread": spread}
 
         def gather_couplings(state):
@@ -248,14 +249,6 @@ def tile_dynamicroutingfusion_pa_kernel(tc, text_feat, vision_proj, Wt, bt, out_
 
         def weigh(g, t, state):
             weighted = results.tile([P, H], F32, tag="weighted")
-            nc.vector.tensor_scalar(
-                out=weighted[:, 0:V_PART],
-                in0=vision_rows[:, g, 0:V_PART],
-                scalar1=state["exp_own"][:, t : t + 1],
-                scalar2=state["inverse_sum"][:, 0:1],
-                op0=ALU.mult,
-                op1=ALU.mult,
-            )
             nc.scalar.activation(
                 out=weighted[:, V_PART:VS_PART],
                 in_=vision_rows[:, g, V_PART:VS_PART],
@@ -320,23 +313,23 @@ def tile_dynamicroutingfusion_pa_kernel(tc, text_feat, vision_proj, Wt, bt, out_
         start_bank(0, 0, 1)
         regroup_unit(4, on_scalar)
         quantise_unit(4)
+        finish_rows(0, 0, 0)
         start_bank(0, 1, 0)
         start_bank(0, 1, 1)
         transpose_unit(5)
-        finish_coupling(0, 0, 0)
-        regroup_unit(5, on_scalar)
-        finish_rows(0, 0, 0)
-        finish_coupling(0, 1, 0)
-        finish_rows(0, 1, 0)
-        finish_coupling(0, 0, 1)
-        quantise_unit(5)
-        start_bank(1, 0, 0)
         finish_rows(0, 0, 1)
-        finish_coupling(0, 1, 1)
+        finish_coupling(0, 0, 0)
+        finish_rows(0, 1, 0)
+        regroup_unit(5, on_scalar)
+        finish_coupling(0, 1, 0)
         finish_rows(0, 1, 1)
+        quantise_unit(5)
+        finish_coupling(0, 0, 1)
+        start_bank(1, 0, 0)
+        start_bank(1, 1, 0)
+        finish_coupling(0, 1, 1)
         vision_bank = spread_vision(1)
         state = spread_couplings(coupling_parts[0])
-        start_bank(1, 1, 0)
         nc.scalar.copy(out=vision_rows[:, 1, :], in_=vision_bank[:])
         gather_couplings(state)
 
@@ -346,28 +339,27 @@ def tile_dynamicroutingfusion_pa_kernel(tc, text_feat, vision_proj, Wt, bt, out_
             if not last:
                 transpose_unit(ahead)
                 vision_bank = spread_vision(g + 1)
+            finish_rows(g, 0, 0)
             finish_coupling(g, 0, 0)
             exponentials(state)
-            if not last:
-                regroup_unit(ahead, on_scalar)
-            finish_rows(g, 0, 0)
             start_bank(g, 0, 1)
-            finish_coupling(g, 1, 0)
             finish_rows(g, 1, 0)
+            finish_coupling(g, 1, 0)
             normalise(state)
             start_bank(g, 1, 1)
-            if not last:
-                quantise_unit(ahead)
-            finish_coupling(g, 0, 1)
-            weigh(g - 1, 0, state)
             finish_rows(g, 0, 1)
+            weigh(g - 1, 0, state)
+            finish_coupling(g, 0, 1)
             if not last:
-                start_bank(g + 1, 0, 0)
-            finish_coupling(g, 1, 1)
-            weigh(g - 1, 1, state)
-            state = spread_couplings(coupling_parts[g])
+                regroup_unit(ahead, on_scalar)
             if not last:
                 finish_rows(g, 1, 1)
+            weigh(g - 1, 1, state)
+            finish_coupling(g, 1, 1)
+            state = spread_couplings(coupling_parts[g])
+            if not last:
+                quantise_unit(ahead)
+                start_bank(g + 1, 0, 0)
                 start_bank(g + 1, 1, 0)
                 nc.scalar.copy(out=vision_rows[:, g + 1, :], in_=vision_bank[:])
             gather_couplings(state)

@@ -26,7 +26,8 @@ HALVES = H // N_HALF
 ROWS = 2
 UNIT = ROWS * P
 V_PART = 0
-VS_PART = 576
+VS_PART = 448
+FIRST_JOINT = 4
 V_BIAS = ((0, 1, 0), (0, 1, 1), (1, 1, 0), (1, 1, 1), (2, 1, 0), (2, 1, 1), (3, 1, 0), (3, 1, 1))
 QUARTERS = P // BATCH
 UNITS = H // UNIT
@@ -41,8 +42,8 @@ def tile_dynamicroutingfusion_pa_kernel(tc, text_feat, vision_proj, Wt, bt, out_
 
     x_dram = text_feat.flatten_outer_dims().rearrange("(g p t) k -> g p t k", p=P, t=ROWS)
     w_dram = Wt.rearrange("(g p t) k -> g p t k", p=P, t=ROWS)
-    proj_dram = out_0.flatten_outer_dims().rearrange("(g p t) h -> g t p h", p=P, t=ROWS)
-    weighted_dram = out_1.flatten_outer_dims().rearrange("(g p t) h -> g t p h", p=P, t=ROWS)
+    proj_dram = out_0.flatten_outer_dims().rearrange("(g p t) h -> g p t h", p=P, t=ROWS)
+    weighted_dram = out_1.flatten_outer_dims().rearrange("(g p t) h -> g p t h", p=P, t=ROWS)
 
     with ExitStack() as ctx:
         keep = ctx.enter_context(tc.tile_pool(name="keep", bufs=1))
@@ -192,21 +193,21 @@ def tile_dynamicroutingfusion_pa_kernel(tc, text_feat, vision_proj, Wt, bt, out_
                 bare = stage.tile([P, N_HALF], F32, tag="bare")
                 nc.scalar.copy(out=bare[:], in_=acc[:])
                 nc.gpsimd.tensor_tensor(out=proj[:, cols], in0=bare[:], in1=bias_rows[:, cols], op=ALU.add)
-            if half == HALVES - 1:
-                nc.sync.dma_start(out=proj_dram[g, t], in_=proj[:])
 
-        def spread_couplings(coupling_parts):
-            coupling = small.tile([P, ROWS], F32, tag="coupling")
-            spread = small.tile([P, ROWS, SHARE], F32, tag="spread")
-            for t in range(ROWS):
-                nc.scalar.activation(
-                    out=coupling[:, t : t + 1],
-                    in_=coupling_parts[:, 0, t : t + 1],
-                    func=ACT.Identity,
-                    bias=coupling_parts[:, 1, t : t + 1],
-                )
-                nc.scalar.activation(out=spread[:, t, :], in_=place_of[:], func=ACT.Copy, scale=coupling[:, t : t + 1])
-            return {"coupling": coupling, "spread": spread}
+        def new_state(g):
+            return {
+                "group": g,
+                "coupling": small.tile([P, ROWS], F32, name="coupling", tag="coupling"),
+                "spread": small.tile([P, ROWS, SHARE], F32, name="spread", tag="spread"),
+            }
+
+        def place_coupling(state, t):
+            parts = coupling_parts[state["group"]]
+            coupling = state["coupling"][:, t : t + 1]
+            nc.scalar.activation(
+                out=coupling, in_=parts[:, 0, t : t + 1], func=ACT.Identity, bias=parts[:, 1, t : t + 1]
+            )
+            nc.scalar.activation(out=state["spread"][:, t, :], in_=place_of[:], func=ACT.Copy, scale=coupling)
 
         def gather_couplings(state):
             batch_couplings = psum_t.tile([P, TOKENS], F32, tag="bank")
@@ -248,7 +249,20 @@ def tile_dynamicroutingfusion_pa_kernel(tc, text_feat, vision_proj, Wt, bt, out_
             state["routing"] = routing
 
         def weigh(g, t, state):
-            weighted = results.tile([P, H], F32, tag="weighted")
+            if t == 0:
+                state["weighted"] = results.tile([P, ROWS, H], F32, name="weighted", tag="weighted", bufs=2)
+            weighted = state["weighted"][:, t, :]
+            if g >= UNITS - 2 and t == 0:
+                nc.vector.tensor_scalar(
+                    out=weighted,
+                    in0=vision_rows[:, g, :],
+                    scalar1=state["exp_own"][:, t : t + 1],
+                    scalar2=state["inverse_sum"][:, 0:1],
+                    op0=ALU.mult,
+                    op1=ALU.mult,
+                )
+                nc.sync.dma_start(out=weighted_dram[g][:, t, :], in_=weighted)
+                return
             nc.scalar.activation(
                 out=weighted[:, V_PART:VS_PART],
                 in_=vision_rows[:, g, V_PART:VS_PART],
@@ -264,7 +278,10 @@ def tile_dynamicroutingfusion_pa_kernel(tc, text_feat, vision_proj, Wt, bt, out_
                     op0=ALU.mult,
                     op1=ALU.mult,
                 )
-            nc.sync.dma_start(out=weighted_dram[g, t], in_=weighted[:])
+            if g >= 0:
+                nc.sync.dma_start(out=weighted_dram[g][:, t, :], in_=weighted)
+            elif t == ROWS - 1:
+                nc.sync.dma_start(out=weighted_dram[g], in_=state["weighted"][:])
 
         proj_tiles = {}
         accs = {}
@@ -277,9 +294,14 @@ def tile_dynamicroutingfusion_pa_kernel(tc, text_feat, vision_proj, Wt, bt, out_
             agree(g, half, t, accs[g, half, t], coupling_parts[g])
 
         def finish_rows(g, half, t):
-            if (g, t) not in proj_tiles:
-                proj_tiles[g, t] = results.tile([P, H], F32, name="proj", tag="proj")
-            add_bias(g, half, t, accs[g, half, t], proj_tiles[g, t], (g, half, t) in V_BIAS)
+            if g not in proj_tiles:
+                proj_tiles[g] = results.tile([P, ROWS, H], F32, name="proj", tag="proj", bufs=3)
+            add_bias(g, half, t, accs[g, half, t], proj_tiles[g][:, t, :], (g, half, t) in V_BIAS)
+            if half == HALVES - 1:
+                if g < FIRST_JOINT:
+                    nc.sync.dma_start(out=proj_dram[g][:, t, :], in_=proj_tiles[g][:, t, :])
+                elif t == ROWS - 1:
+                    nc.sync.dma_start(out=proj_dram[g], in_=proj_tiles[g][:])
 
         def transpose_unit(n):
             for c in range(PASSES):
@@ -297,74 +319,97 @@ def tile_dynamicroutingfusion_pa_kernel(tc, text_feat, vision_proj, Wt, bt, out_
         grouped = {}
         on_scalar = (nc.scalar.copy, nc.scalar.copy)
         on_both = (nc.scalar.copy, nc.vector.tensor_copy)
-        vision_bank = spread_vision(0)
-        bias_bank = spread_bias()
-        nc.scalar.copy(out=vision_rows[:, 0, :], in_=vision_bank[:])
-        nc.scalar.copy(out=bias_rows[:], in_=bias_bank[:])
-        for n in (0, 1, 2):
-            transpose_unit(n)
-            regroup_unit(n, on_both)
-            quantise_unit(n)
-        transpose_unit(3)
-        regroup_unit(3, on_scalar)
-        transpose_unit(4)
-        quantise_unit(3)
-        start_bank(0, 0, 0)
-        start_bank(0, 0, 1)
-        regroup_unit(4, on_scalar)
-        quantise_unit(4)
-        finish_rows(0, 0, 0)
-        start_bank(0, 1, 0)
-        start_bank(0, 1, 1)
-        transpose_unit(5)
-        finish_rows(0, 0, 1)
-        finish_coupling(0, 0, 0)
-        finish_rows(0, 1, 0)
-        regroup_unit(5, on_scalar)
-        finish_coupling(0, 1, 0)
-        finish_rows(0, 1, 1)
-        quantise_unit(5)
-        finish_coupling(0, 0, 1)
-        start_bank(1, 0, 0)
-        start_bank(1, 1, 0)
-        finish_coupling(0, 1, 1)
-        vision_bank = spread_vision(1)
-        state = spread_couplings(coupling_parts[0])
-        nc.scalar.copy(out=vision_rows[:, 1, :], in_=vision_bank[:])
-        gather_couplings(state)
+        with tc.manual_schedule():
+            vision_bank = spread_vision(0)
+            bias_bank = spread_bias()
+            nc.scalar.copy(out=vision_rows[:, 0, :], in_=vision_bank[:])
+            nc.scalar.copy(out=bias_rows[:], in_=bias_bank[:])
+            for n in (0, 1, 2):
+                transpose_unit(n)
+                regroup_unit(n, on_both)
+                quantise_unit(n)
+            transpose_unit(3)
+            regroup_unit(3, on_scalar)
+            transpose_unit(4)
+            quantise_unit(3)
+            start_bank(0, 0, 0)
+            start_bank(0, 0, 1)
+            regroup_unit(4, on_scalar)
+            quantise_unit(4)
+            start_bank(0, 1, 0)
+            transpose_unit(5)
+            start_bank(0, 1, 1)
+            vision_bank = spread_vision(1)
+            finish_rows(0, 0, 0)
+            finish_rows(0, 0, 1)
+            finish_coupling(0, 0, 0)
+            finish_rows(0, 1, 0)
+            finish_coupling(0, 0, 1)
+            regroup_unit(5, on_scalar)
+            finish_coupling(0, 1, 0)
+            nc.scalar.copy(out=vision_rows[:, 1, :], in_=vision_bank[:])
+            quantise_unit(5)
+            finish_rows(0, 1, 1)
+            start_bank(1, 0, 0)
+            state = new_state(0)
+            place_coupling(state, 0)
+            finish_coupling(0, 1, 1)
+            start_bank(1, 1, 0)
+            transpose_unit(6)
 
-        for g in range(1, UNITS):
-            last = g == UNITS - 1
-            ahead = 1 + UNITS + g
-            if not last:
-                transpose_unit(ahead)
+            for g in range(1, UNITS - 1):
+                ahead = 1 + UNITS + g
+                finish_rows(g, 0, 0)
+                place_coupling(state, 1)
+                gather_couplings(state)
+                finish_rows(g, 1, 0)
+                finish_coupling(g, 0, 0)
+                regroup_unit(ahead, on_scalar)
+                exponentials(state)
+                start_bank(g, 0, 1)
+                start_bank(g, 1, 1)
                 vision_bank = spread_vision(g + 1)
+                finish_rows(g, 0, 1)
+                finish_coupling(g, 1, 0)
+                normalise(state)
+                quantise_unit(ahead)
+                start_bank(g + 1, 0, 0)
+                finish_rows(g, 1, 1)
+                start_bank(g + 1, 1, 0)
+                if ahead + 1 < 2 * UNITS:
+                    transpose_unit(ahead + 1)
+                next_state = new_state(g)
+                place_coupling(next_state, 0)
+                nc.scalar.copy(out=vision_rows[:, g + 1, :], in_=vision_bank[:])
+                for t in range(ROWS):
+                    weigh(g - 1, t, state)
+                state = next_state
+                finish_coupling(g, 0, 1)
+                finish_coupling(g, 1, 1)
+
+            g = UNITS - 1
             finish_rows(g, 0, 0)
+            place_coupling(state, 1)
+            gather_couplings(state)
+            finish_rows(g, 1, 0)
             finish_coupling(g, 0, 0)
             exponentials(state)
             start_bank(g, 0, 1)
-            finish_rows(g, 1, 0)
+            start_bank(g, 1, 1)
             finish_coupling(g, 1, 0)
             normalise(state)
-            start_bank(g, 1, 1)
+            for t in range(ROWS):
+                weigh(g - 1, t, state)
             finish_rows(g, 0, 1)
-            weigh(g - 1, 0, state)
-            finish_coupling(g, 0, 1)
-            if not last:
-                regroup_unit(ahead, on_scalar)
-            if not last:
-                finish_rows(g, 1, 1)
-            weigh(g - 1, 1, state)
+            next_state = new_state(g)
+            place_coupling(next_state, 0)
             finish_coupling(g, 1, 1)
-            state = spread_couplings(coupling_parts[g])
-            if not last:
-                quantise_unit(ahead)
-                start_bank(g + 1, 0, 0)
-                start_bank(g + 1, 1, 0)
-                nc.scalar.copy(out=vision_rows[:, g + 1, :], in_=vision_bank[:])
+            finish_coupling(g, 0, 1)
+            state = next_state
+            place_coupling(state, 1)
             gather_couplings(state)
-        finish_rows(UNITS - 1, 1, 1)
-        exponentials(state)
-        normalise(state)
-        for t in range(ROWS):
-            weigh(UNITS - 1, t, state)
+            finish_rows(g, 1, 1)
+            exponentials(state)
+            normalise(state)
+            for t in range(ROWS):
+                weigh(g, t, state)

@@ -321,9 +321,7 @@ def tile_dynamicroutingfusion_pa_kernel(tc, text_feat, vision_proj, Wt, bt, out_
         on_both = (nc.scalar.copy, nc.vector.tensor_copy)
         with tc.manual_schedule():
             vision_bank = spread_vision(0)
-            bias_bank = spread_bias()
             nc.scalar.copy(out=vision_rows[:, 0, :], in_=vision_bank[:])
-            nc.scalar.copy(out=bias_rows[:], in_=bias_bank[:])
             for n in (0, 1, 2):
                 transpose_unit(n)
                 regroup_unit(n, on_both)
@@ -332,23 +330,25 @@ def tile_dynamicroutingfusion_pa_kernel(tc, text_feat, vision_proj, Wt, bt, out_
             regroup_unit(3, on_scalar)
             transpose_unit(4)
             quantise_unit(3)
+            bias_bank = spread_bias()
             start_bank(0, 0, 0)
             start_bank(0, 0, 1)
             regroup_unit(4, on_scalar)
+            nc.scalar.copy(out=bias_rows[:], in_=bias_bank[:])
             quantise_unit(4)
             start_bank(0, 1, 0)
             transpose_unit(5)
             start_bank(0, 1, 1)
             vision_bank = spread_vision(1)
-            finish_rows(0, 0, 0)
-            finish_rows(0, 0, 1)
             finish_coupling(0, 0, 0)
-            finish_rows(0, 1, 0)
+            finish_rows(0, 0, 0)
             finish_coupling(0, 0, 1)
+            finish_rows(0, 1, 0)
             regroup_unit(5, on_scalar)
             finish_coupling(0, 1, 0)
-            nc.scalar.copy(out=vision_rows[:, 1, :], in_=vision_bank[:])
             quantise_unit(5)
+            finish_rows(0, 0, 1)
+            nc.scalar.copy(out=vision_rows[:, 1, :], in_=vision_bank[:])
             finish_rows(0, 1, 1)
             start_bank(1, 0, 0)
             state = new_state(0)

@@ -26,8 +26,9 @@ HALVES = H // N_HALF
 ROWS = 2
 UNIT = ROWS * P
 V_PART = 0
-VS_PART = 448
+VS_PART = 320
 FIRST_JOINT = 4
+LAST_V = 640
 V_BIAS = ((0, 1, 0), (0, 1, 1), (1, 1, 0), (1, 1, 1), (2, 1, 0), (2, 1, 1), (3, 1, 0), (3, 1, 1))
 QUARTERS = P // BATCH
 UNITS = H // UNIT
@@ -252,15 +253,23 @@ def tile_dynamicroutingfusion_pa_kernel(tc, text_feat, vision_proj, Wt, bt, out_
             if t == 0:
                 state["weighted"] = results.tile([P, ROWS, H], F32, name="weighted", tag="weighted", bufs=2)
             weighted = state["weighted"][:, t, :]
-            if g >= UNITS - 2 and t == 0:
+            by_vector = H if g == UNITS - 2 and t == 0 else LAST_V if g == UNITS - 1 else 0
+            if by_vector > 0:
                 nc.vector.tensor_scalar(
-                    out=weighted,
-                    in0=vision_rows[:, g, :],
+                    out=weighted[:, 0:by_vector],
+                    in0=vision_rows[:, g, 0:by_vector],
                     scalar1=state["exp_own"][:, t : t + 1],
                     scalar2=state["inverse_sum"][:, 0:1],
                     op0=ALU.mult,
                     op1=ALU.mult,
                 )
+                if by_vector < H:
+                    nc.scalar.activation(
+                        out=weighted[:, by_vector:H],
+                        in_=vision_rows[:, g, by_vector:H],
+                        func=ACT.Copy,
+                        scale=state["routing"][:, t : t + 1],
+                    )
                 nc.sync.dma_start(out=weighted_dram[g][:, t, :], in_=weighted)
                 return
             nc.scalar.activation(

@@ -23,17 +23,19 @@ WORDS = K_PASS // 2
 N_HALF = 512
 HALVES = H // N_HALF
 
+FIRST_TILES = 2
+V_BIAS = tuple((n, 1) for n in range(8))
+VS_PART = 320
+VECTOR_WEIGHS = {(2, 0): H, (3, 0): 640, (4, 0): 640}
+QUARTERS = P // BATCH
 ROWS = 2
 UNIT = ROWS * P
-V_PART = 0
-VS_PART = 320
-FIRST_JOINT = 4
-LAST_V = 640
-V_BIAS = ((0, 1, 0), (0, 1, 1), (1, 1, 0), (1, 1, 1), (2, 1, 0), (2, 1, 1), (3, 1, 0), (3, 1, 1))
-QUARTERS = P // BATCH
 UNITS = H // UNIT
-BATCHES = UNIT // TOKENS
-SHARE = P // BATCHES
+GROUP_TILES = (2, 2, 2, 1, 1)
+GROUPS = len(GROUP_TILES)
+TILE_LIST = [(g, t) for g, tiles in enumerate(GROUP_TILES) for t in range(tiles)]
+FIRST_TILE = [sum(GROUP_TILES[:g]) for g in range(GROUPS)]
+BATCHES_PER_TILE = P // TOKENS
 
 FLOPS = 2 * BATCH * TOKENS * H * H
 
@@ -41,10 +43,18 @@ FLOPS = 2 * BATCH * TOKENS * H * H
 def tile_dynamicroutingfusion_pa_kernel(tc, text_feat, vision_proj, Wt, bt, out_0, out_1):
     nc = tc.nc
 
-    x_dram = text_feat.flatten_outer_dims().rearrange("(g p t) k -> g p t k", p=P, t=ROWS)
+    def tokens_of(dram):
+        flat = dram.flatten_outer_dims()
+        views = []
+        for g, tiles in enumerate(GROUP_TILES):
+            first = FIRST_TILE[g] * P
+            views.append(flat[first : first + tiles * P, :].rearrange("(p t) k -> p t k", t=tiles))
+        return views
+
+    x_dram = tokens_of(text_feat)
+    proj_dram = tokens_of(out_0)
+    weighted_dram = tokens_of(out_1)
     w_dram = Wt.rearrange("(g p t) k -> g p t k", p=P, t=ROWS)
-    proj_dram = out_0.flatten_outer_dims().rearrange("(g p t) h -> g p t h", p=P, t=ROWS)
-    weighted_dram = out_1.flatten_outer_dims().rearrange("(g p t) h -> g p t h", p=P, t=ROWS)
 
     with ExitStack() as ctx:
         keep = ctx.enter_context(tc.tile_pool(name="keep", bufs=1))
@@ -55,7 +65,7 @@ def tile_dynamicroutingfusion_pa_kernel(tc, text_feat, vision_proj, Wt, bt, out_
         psum_acc = ctx.enter_context(tc.psum_pool(name="psum_acc", bufs=4))
 
         raw = {
-            "x": keep.tile([P, UNITS, ROWS, H], BF16, name="x_raw"),
+            "x": keep.tile([P, len(TILE_LIST), H], BF16, name="x_raw"),
             "w": keep.tile([P, UNITS, ROWS, H], BF16, name="w_raw"),
         }
         codes = {
@@ -66,87 +76,107 @@ def tile_dynamicroutingfusion_pa_kernel(tc, text_feat, vision_proj, Wt, bt, out_
             "x": keep.tile([P, PASSES, H], U8, name="x_scales", align_bytes=64),
             "w": keep.tile([P, PASSES, H], U8, name="w_scales", align_bytes=64),
         }
-        vision_rows = keep.tile([P, UNITS, H], BF16)
+        vision_rows = keep.tile([P, GROUPS, H], BF16)
         vision_seed = keep.tile([P, H // QUARTERS], BF16)
         bias_seed = keep.tile([P, H], BF16)
         bias_rows = keep.tile([P, H], BF16)
 
+        ones = keep.tile([P, P], BF16)
+        nc.vector.memset(ones[:], 1.0)
         nc.vector.memset(bias_seed[:].bitcast(F32), 0.0)
         nc.sync.dma_start(
             out=vision_seed[:], in_=vision_proj.flatten_outer_dims().rearrange("b (q h) -> (b q) h", q=QUARTERS)
         )
         nc.sync.dma_start(out=bias_seed[0:1, :], in_=bt.unsqueeze(0))
-        order = [("x", 0)] + [("w", u) for u in range(UNITS)] + [("x", u) for u in range(1, UNITS)]
-        dram = {"x": x_dram, "w": w_dram}
-        for operand, unit in order:
-            nc.sync.dma_start(out=raw[operand][:, unit, :, :], in_=dram[operand][unit])
+
+        def load_tokens(g, first, end):
+            tile = FIRST_TILE[g]
+            nc.sync.dma_start(out=raw["x"][:, tile + first : tile + end, :], in_=x_dram[g][:, first:end, :])
+
+        load_tokens(0, 0, FIRST_TILES)
+        for u in range(UNITS):
+            nc.sync.dma_start(out=raw["w"][:, u, :, :], in_=w_dram[u])
+        if FIRST_TILES < GROUP_TILES[0]:
+            load_tokens(0, FIRST_TILES, GROUP_TILES[0])
+        for g in range(1, GROUPS):
+            for first in range(0, GROUP_TILES[g], 2):
+                load_tokens(g, first, min(first + 2, GROUP_TILES[g]))
 
         ident = keep.tile([P, P], F32)
         make_identity(nc, ident[:])
-        pick = keep.tile([P, QUARTERS, BATCH, SHARE], BF16)
-        for first, end in ((0, BATCHES), (BATCHES, BATCH)):
+        quarter_of = ident[:].rearrange("p (b q) -> p q b", q=QUARTERS)
+        pick = []
+        for g, tiles in enumerate(GROUP_TILES):
+            batches = tiles * BATCHES_PER_TILE
+            first = FIRST_TILE[g] * BATCHES_PER_TILE
+            pick.append(keep.tile([P, QUARTERS, batches, P // batches], BF16, name="pick", tag="pick%d" % g))
             nc.vector.tensor_copy(
-                out=pick[:, :, first:end, :],
-                in_=ident[:]
-                .rearrange("p (b q) -> p q b", q=QUARTERS)[:, :, first:end]
-                .unsqueeze(3)
-                .to_broadcast([P, QUARTERS, end - first, SHARE]),
+                out=pick[g][:],
+                in_=quarter_of[:, :, first : first + batches].unsqueeze(3).to_broadcast([P, QUARTERS, batches, P // batches]),
             )
-        ones = keep.tile([P, P], BF16)
-        nc.vector.memset(ones[:], 1.0)
         warm = keep.tile([P, 1], F32)
         nc.vector.memset(warm[:], 0.0)
         nc.scalar.activation(out=warm[:], in_=warm[:], func=ACT.Exp)
-        batch_of = keep.tile([P, BATCHES], F32)
-        nc.vector.tensor_reduce(
-            out=batch_of[:], in_=ident[:].rearrange("p (b j) -> p b j", j=SHARE), axis=AXIS.X, op=ALU.add
-        )
-        same_batch = keep.tile([P, P], F32)
-        nc.vector.tensor_copy(
-            out=same_batch[:].rearrange("p (b j) -> p b j", j=SHARE),
-            in_=batch_of[:].unsqueeze(2).to_broadcast([P, BATCHES, SHARE]),
-        )
-        place_of = keep.tile([P, SHARE], F32)
-        nc.vector.tensor_reduce(
-            out=place_of[:], in_=ident[:].rearrange("p (b j) -> p j b", j=SHARE), axis=AXIS.X, op=ALU.add
-        )
+        same_batch = {}
+        place_of = {}
+        for tiles in sorted(set(GROUP_TILES)):
+            batches = tiles * BATCHES_PER_TILE
+            share = P // batches
+            batch_of = keep.tile([P, batches], F32, name="batch_of", tag="batch_of%d" % tiles)
+            nc.vector.tensor_reduce(
+                out=batch_of[:], in_=ident[:].rearrange("p (b j) -> p b j", j=share), axis=AXIS.X, op=ALU.add
+            )
+            same_batch[tiles] = keep.tile([P, P], F32, name="same_batch", tag="same_batch%d" % tiles)
+            nc.vector.tensor_copy(
+                out=same_batch[tiles][:].rearrange("p (b j) -> p b j", j=share),
+                in_=batch_of[:].unsqueeze(2).to_broadcast([P, batches, share]),
+            )
+            place_of[tiles] = keep.tile([P, share], F32, name="place_of", tag="place_of%d" % tiles)
+            nc.vector.tensor_reduce(
+                out=place_of[tiles][:], in_=ident[:].rearrange("p (b j) -> p j b", j=share), axis=AXIS.X, op=ALU.add
+            )
 
-        steps = [(operand, unit, c) for operand, unit in order for c in range(PASSES)]
+        def pick_words(rows, c, u):
+            return rows.bitcast(F32)[:, c * WORDS + u : (c + 1) * WORDS : 2]
 
-        def transpose(step):
-            operand, unit, c = steps[step]
-            bank = psum_t.tile([P, 2, ROWS, P], F32, tag="bank")
-            for t in range(ROWS):
-                words = raw[operand][:, unit, t, :].bitcast(F32)
+        def transpose_tokens(g, t):
+            bank = psum_t.tile([P, PASSES, 2, P], F32, tag="bank")
+            for c in range(PASSES):
                 for u in range(2):
-                    nc.tensor.transpose(bank[:, u, t, :], words[:, c * WORDS + u : (c + 1) * WORDS : 2], ident[:])
+                    nc.tensor.transpose(bank[:, c, u, :], pick_words(raw["x"][:, FIRST_TILE[g] + t, :], c, u), ident[:])
             return bank
 
-        def regroup(step, bank, copy):
-            operand, unit, c = steps[step]
+        def transpose_weights(n, c):
+            bank = psum_t.tile([P, 2, ROWS, P], F32, tag="bank")
+            for t in range(ROWS):
+                for u in range(2):
+                    nc.tensor.transpose(bank[:, u, t, :], pick_words(raw["w"][:, n, t, :], c, u), ident[:])
+            return bank
+
+        def regroup_tokens(bank, copy):
             grouped = stage.tile([P, UNIT * 4], BF16, align_bytes=64, tag="grouped")
-            if operand == "x":
-                out = grouped[:].bitcast(F32).rearrange("p (t r u) -> p t r u", t=ROWS, u=2)
-                in_ = bank[:].rearrange("p u t r -> p t r u")
-            else:
-                out = grouped[:].bitcast(F32).rearrange("p (r t u) -> p r t u", t=ROWS, u=2)
-                in_ = bank[:].rearrange("p u t r -> p r t u")
-            copy(out=out, in_=in_)
+            out = grouped[:].bitcast(F32).rearrange("p (c r u) -> p c r u", c=PASSES, u=2)
+            copy(out=out, in_=bank[:].rearrange("p c u r -> p c r u"))
             return grouped
 
-        def quantise(step, grouped):
-            operand, unit, c = steps[step]
+        def regroup_weights(bank, copy):
+            grouped = stage.tile([P, UNIT * 4], BF16, align_bytes=64, tag="grouped")
+            out = grouped[:].bitcast(F32).rearrange("p (r t u) -> p r t u", t=ROWS, u=2)
+            copy(out=out, in_=bank[:].rearrange("p u t r -> p r t u"))
+            return grouped
+
+        def quantise(operand, c, first, width, in_):
             nc.vector.quantize_mx(
-                out=codes[operand][:, c, unit * UNIT : (unit + 1) * UNIT].bitcast(FP8X4),
-                scales=scales[operand][:, c, unit * UNIT : (unit + 1) * UNIT],
-                in_=grouped[:],
+                out=codes[operand][:, c, first : first + width].bitcast(FP8X4),
+                scales=scales[operand][:, c, first : first + width],
+                in_=in_,
             )
 
         def spread_vision(g):
             bank = psum_t.tile([P, H], BF16, tag="bank")
             width = H // QUARTERS
             for q in range(QUARTERS):
-                lhsT = pick[:, q, g * BATCHES : (g + 1) * BATCHES, :].rearrange("p b j -> p (b j)")
+                lhsT = pick[g][:, q, :, :].rearrange("p b j -> p (b j)")
                 cols = slice(q * width, (q + 1) * width)
                 nc.tensor.matmul(out=bank[:, cols], lhsT=lhsT, rhs=vision_seed[:], start=True, stop=True)
             return bank
@@ -159,7 +189,7 @@ def tile_dynamicroutingfusion_pa_kernel(tc, text_feat, vision_proj, Wt, bt, out_
             return bank
 
         def multiply(g, half, t):
-            first = g * UNIT + t * P
+            first = (FIRST_TILE[g] + t) * P
             acc = psum_acc.tile([P, N_HALF], F32)
             for c in range(PASSES):
                 nc.tensor.matmul_mx(
@@ -194,12 +224,13 @@ def tile_dynamicroutingfusion_pa_kernel(tc, text_feat, vision_proj, Wt, bt, out_
                 bare = stage.tile([P, N_HALF], F32, tag="bare")
                 nc.scalar.copy(out=bare[:], in_=acc[:])
                 nc.gpsimd.tensor_tensor(out=proj[:, cols], in0=bare[:], in1=bias_rows[:, cols], op=ALU.add)
-
         def new_state(g):
+            tiles = GROUP_TILES[g]
             return {
                 "group": g,
-                "coupling": small.tile([P, ROWS], F32, name="coupling", tag="coupling"),
-                "spread": small.tile([P, ROWS, SHARE], F32, name="spread", tag="spread"),
+                "tiles": tiles,
+                "coupling": small.tile([P, tiles], F32, name="coupling", tag="coupling"),
+                "spread": small.tile([P, tiles, TOKENS // tiles], F32, name="spread", tag="spread"),
             }
 
         def place_coupling(state, t):
@@ -208,18 +239,19 @@ def tile_dynamicroutingfusion_pa_kernel(tc, text_feat, vision_proj, Wt, bt, out_
             nc.scalar.activation(
                 out=coupling, in_=parts[:, 0, t : t + 1], func=ACT.Identity, bias=parts[:, 1, t : t + 1]
             )
-            nc.scalar.activation(out=state["spread"][:, t, :], in_=place_of[:], func=ACT.Copy, scale=coupling)
+            nc.scalar.activation(
+                out=state["spread"][:, t, :], in_=place_of[state["tiles"]][:], func=ACT.Copy, scale=coupling
+            )
 
         def gather_couplings(state):
-            batch_couplings = psum_t.tile([P, TOKENS], F32, tag="bank")
+            state["batch_couplings"] = psum_t.tile([P, TOKENS], F32, name="batch_couplings", tag="bank")
             nc.tensor.matmul(
-                out=batch_couplings[:],
-                lhsT=same_batch[:],
+                out=state["batch_couplings"][:],
+                lhsT=same_batch[state["tiles"]][:],
                 rhs=state["spread"][:].rearrange("p t j -> p (t j)"),
                 start=True,
                 stop=True,
             )
-            state["batch_couplings"] = batch_couplings
 
         def exponentials(state):
             minus_max = small.tile([P, 1], F32, tag="minus_max")
@@ -236,7 +268,7 @@ def tile_dynamicroutingfusion_pa_kernel(tc, text_feat, vision_proj, Wt, bt, out_
                 scale=1.0,
                 accum_out=exp_sum[:],
             )
-            exp_own = small.tile([P, ROWS], F32, tag="exp_own")
+            exp_own = small.tile([P, state["tiles"]], F32, name="exp_own", tag="exp_own%d" % state["tiles"])
             nc.scalar.activation(out=exp_own[:], in_=state["coupling"][:], func=ACT.Exp, bias=minus_max[:], scale=1.0)
             state["exp_sum"] = exp_sum
             state["exp_own"] = exp_own
@@ -244,16 +276,14 @@ def tile_dynamicroutingfusion_pa_kernel(tc, text_feat, vision_proj, Wt, bt, out_
         def normalise(state):
             inverse_sum = small.tile([P, 1], F32, tag="inverse_sum")
             nc.vector.reciprocal(out=inverse_sum[:], in_=state["exp_sum"][:])
-            routing = small.tile([P, ROWS], F32, tag="routing")
+            routing = small.tile([P, state["tiles"]], F32, name="routing", tag="routing%d" % state["tiles"])
             nc.scalar.activation(out=routing[:], in_=state["exp_own"][:], func=ACT.Copy, scale=inverse_sum[:])
             state["inverse_sum"] = inverse_sum
             state["routing"] = routing
 
         def weigh(g, t, state):
-            if t == 0:
-                state["weighted"] = results.tile([P, ROWS, H], F32, name="weighted", tag="weighted", bufs=2)
-            weighted = state["weighted"][:, t, :]
-            by_vector = H if g == UNITS - 2 and t == 0 else LAST_V if g == UNITS - 1 else 0
+            weighted = results.tile([P, H], F32, name="weighted", tag="weighted", bufs=5)
+            by_vector = VECTOR_WEIGHS.get((g, t), 0)
             if by_vector > 0:
                 nc.vector.tensor_scalar(
                     out=weighted[:, 0:by_vector],
@@ -263,162 +293,184 @@ def tile_dynamicroutingfusion_pa_kernel(tc, text_feat, vision_proj, Wt, bt, out_
                     op0=ALU.mult,
                     op1=ALU.mult,
                 )
-                if by_vector < H:
-                    nc.scalar.activation(
-                        out=weighted[:, by_vector:H],
-                        in_=vision_rows[:, g, by_vector:H],
-                        func=ACT.Copy,
-                        scale=state["routing"][:, t : t + 1],
-                    )
-                nc.sync.dma_start(out=weighted_dram[g][:, t, :], in_=weighted)
-                return
-            nc.scalar.activation(
-                out=weighted[:, V_PART:VS_PART],
-                in_=vision_rows[:, g, V_PART:VS_PART],
-                func=ACT.Copy,
-                scale=state["routing"][:, t : t + 1],
-            )
-            if VS_PART < H:
+            by_scalar = H if by_vector > 0 else VS_PART
+            if by_vector < by_scalar:
+                nc.scalar.activation(
+                    out=weighted[:, by_vector:by_scalar],
+                    in_=vision_rows[:, g, by_vector:by_scalar],
+                    func=ACT.Copy,
+                    scale=state["routing"][:, t : t + 1],
+                )
+            if by_scalar < H:
                 nc.gpsimd.tensor_scalar(
-                    out=weighted[:, VS_PART:H],
-                    in0=vision_rows[:, g, VS_PART:H],
+                    out=weighted[:, by_scalar:H],
+                    in0=vision_rows[:, g, by_scalar:H],
                     scalar1=state["exp_own"][:, t : t + 1],
                     scalar2=state["inverse_sum"][:, 0:1],
                     op0=ALU.mult,
                     op1=ALU.mult,
                 )
-            if g >= 0:
-                nc.sync.dma_start(out=weighted_dram[g][:, t, :], in_=weighted)
-            elif t == ROWS - 1:
-                nc.sync.dma_start(out=weighted_dram[g], in_=state["weighted"][:])
+            nc.sync.dma_start(out=weighted_dram[g][:, t, :], in_=weighted[:])
 
         proj_tiles = {}
         accs = {}
-        coupling_parts = [small.tile([P, HALVES, ROWS], F32, name="coupling_parts") for g in range(UNITS)]
+        coupling_parts = [
+            small.tile([P, HALVES, tiles], F32, name="coupling_parts", tag="coupling_parts%d" % g, bufs=1)
+            for g, tiles in enumerate(GROUP_TILES)
+        ]
 
-        def start_bank(g, half, t):
-            accs[g, half, t] = multiply(g, half, t)
+        def start_bank(n, half):
+            accs[n, half] = multiply(TILE_LIST[n][0], half, TILE_LIST[n][1])
 
-        def finish_coupling(g, half, t):
-            agree(g, half, t, accs[g, half, t], coupling_parts[g])
+        def finish_coupling(n, half):
+            g, t = TILE_LIST[n]
+            agree(g, half, t, accs[n, half], coupling_parts[g])
 
-        def finish_rows(g, half, t):
-            if g not in proj_tiles:
-                proj_tiles[g] = results.tile([P, ROWS, H], F32, name="proj", tag="proj", bufs=3)
-            add_bias(g, half, t, accs[g, half, t], proj_tiles[g][:, t, :], (g, half, t) in V_BIAS)
+        def finish_rows(n, half):
+            g, t = TILE_LIST[n]
+            if n not in proj_tiles:
+                proj_tiles[n] = results.tile([P, H], F32, name="proj", tag="proj", bufs=4)
+            add_bias(g, half, t, accs[n, half], proj_tiles[n], (n, half) in V_BIAS)
             if half == HALVES - 1:
-                if g < FIRST_JOINT:
-                    nc.sync.dma_start(out=proj_dram[g][:, t, :], in_=proj_tiles[g][:, t, :])
-                elif t == ROWS - 1:
-                    nc.sync.dma_start(out=proj_dram[g], in_=proj_tiles[g][:])
+                nc.sync.dma_start(out=proj_dram[g][:, t, :], in_=proj_tiles[n][:])
 
-        def transpose_unit(n):
-            for c in range(PASSES):
-                transposed[n, c] = transpose(n * PASSES + c)
-
-        def regroup_unit(n, copies):
-            for c in range(PASSES):
-                grouped[n, c] = regroup(n * PASSES + c, transposed[n, c], copies[c])
-
-        def quantise_unit(n):
-            for c in range(PASSES):
-                quantise(n * PASSES + c, grouped[n, c])
-
-        transposed = {}
+        banks = {}
         grouped = {}
+
+        def transpose_x(n):
+            banks[n] = transpose_tokens(*TILE_LIST[n])
+
+        def regroup_x(n, copy):
+            grouped[n] = regroup_tokens(banks[n], copy)
+
+        def quantise_x(n):
+            for c in range(PASSES):
+                quantise("x", c, n * P, P, grouped[n][:, c * P * 4 : (c + 1) * P * 4])
+
+        def transpose_w(n):
+            for c in range(PASSES):
+                banks["w", n, c] = transpose_weights(n, c)
+
+        def regroup_w(n, copies):
+            for c in range(PASSES):
+                grouped["w", n, c] = regroup_weights(banks["w", n, c], copies[c])
+
+        def quantise_w(n):
+            for c in range(PASSES):
+                quantise("w", c, n * UNIT, UNIT, grouped["w", n, c][:])
+
         on_scalar = (nc.scalar.copy, nc.scalar.copy)
         on_both = (nc.scalar.copy, nc.vector.tensor_copy)
         with tc.manual_schedule():
             vision_bank = spread_vision(0)
             nc.scalar.copy(out=vision_rows[:, 0, :], in_=vision_bank[:])
-            for n in (0, 1, 2):
-                transpose_unit(n)
-                regroup_unit(n, on_both)
-                quantise_unit(n)
-            transpose_unit(3)
-            regroup_unit(3, on_scalar)
-            transpose_unit(4)
-            quantise_unit(3)
+            transpose_x(0)
+            transpose_x(1)
+            regroup_x(0, nc.scalar.copy)
+            regroup_x(1, nc.vector.tensor_copy)
+            quantise_x(0)
+            quantise_x(1)
+            transpose_w(0)
+            regroup_w(0, on_both)
+            quantise_w(0)
+            transpose_w(1)
+            regroup_w(1, on_both)
+            quantise_w(1)
+            transpose_w(2)
+            regroup_w(2, on_scalar)
+            transpose_w(3)
+            quantise_w(2)
             bias_bank = spread_bias()
-            start_bank(0, 0, 0)
-            start_bank(0, 0, 1)
-            regroup_unit(4, on_scalar)
+            start_bank(0, 0)
+            start_bank(1, 0)
+            regroup_w(3, on_scalar)
             nc.scalar.copy(out=bias_rows[:], in_=bias_bank[:])
-            quantise_unit(4)
-            start_bank(0, 1, 0)
-            transpose_unit(5)
-            start_bank(0, 1, 1)
+            quantise_w(3)
+            start_bank(0, 1)
+            transpose_x(2)
+            transpose_x(3)
+            start_bank(1, 1)
             vision_bank = spread_vision(1)
-            finish_coupling(0, 0, 0)
-            finish_rows(0, 0, 0)
-            finish_coupling(0, 0, 1)
-            finish_rows(0, 1, 0)
-            regroup_unit(5, on_scalar)
-            finish_coupling(0, 1, 0)
-            quantise_unit(5)
-            finish_rows(0, 0, 1)
+            finish_coupling(0, 0)
+            finish_rows(0, 0)
+            finish_coupling(1, 0)
+            finish_rows(0, 1)
+            regroup_x(2, nc.scalar.copy)
+            regroup_x(3, nc.scalar.copy)
+            finish_coupling(0, 1)
+            quantise_x(2)
+            quantise_x(3)
+            finish_rows(1, 0)
             nc.scalar.copy(out=vision_rows[:, 1, :], in_=vision_bank[:])
-            finish_rows(0, 1, 1)
-            start_bank(1, 0, 0)
+            finish_rows(1, 1)
+            start_bank(2, 0)
             state = new_state(0)
             place_coupling(state, 0)
-            finish_coupling(0, 1, 1)
-            start_bank(1, 1, 0)
-            transpose_unit(6)
+            finish_coupling(1, 1)
+            start_bank(2, 1)
+            transpose_x(4)
+            transpose_x(5)
 
-            for g in range(1, UNITS - 1):
-                ahead = 1 + UNITS + g
-                finish_rows(g, 0, 0)
+            for g in (1, 2):
+                n = 2 * g
+                finish_rows(n, 0)
                 place_coupling(state, 1)
                 gather_couplings(state)
-                finish_rows(g, 1, 0)
-                finish_coupling(g, 0, 0)
-                regroup_unit(ahead, on_scalar)
+                finish_rows(n, 1)
+                finish_coupling(n, 0)
+                regroup_x(n + 2, nc.scalar.copy)
+                regroup_x(n + 3, nc.scalar.copy)
                 exponentials(state)
-                start_bank(g, 0, 1)
-                start_bank(g, 1, 1)
+                start_bank(n + 1, 0)
+                start_bank(n + 1, 1)
                 vision_bank = spread_vision(g + 1)
-                finish_rows(g, 0, 1)
-                finish_coupling(g, 1, 0)
+                finish_rows(n + 1, 0)
+                finish_coupling(n, 1)
                 normalise(state)
-                quantise_unit(ahead)
-                start_bank(g + 1, 0, 0)
-                finish_rows(g, 1, 1)
-                start_bank(g + 1, 1, 0)
-                if ahead + 1 < 2 * UNITS:
-                    transpose_unit(ahead + 1)
+                quantise_x(n + 2)
+                quantise_x(n + 3)
+                start_bank(n + 2, 0)
+                finish_rows(n + 1, 1)
+                start_bank(n + 2, 1)
+                if g == 1:
+                    transpose_x(n + 4)
+                    transpose_x(n + 5)
                 next_state = new_state(g)
                 place_coupling(next_state, 0)
                 nc.scalar.copy(out=vision_rows[:, g + 1, :], in_=vision_bank[:])
-                for t in range(ROWS):
+                for t in range(2):
                     weigh(g - 1, t, state)
                 state = next_state
-                finish_coupling(g, 0, 1)
-                finish_coupling(g, 1, 1)
+                finish_coupling(n + 1, 0)
+                finish_coupling(n + 1, 1)
 
-            g = UNITS - 1
-            finish_rows(g, 0, 0)
+            finish_rows(6, 0)
             place_coupling(state, 1)
             gather_couplings(state)
-            finish_rows(g, 1, 0)
-            finish_coupling(g, 0, 0)
+            vision_bank = spread_vision(4)
+            finish_rows(6, 1)
+            finish_coupling(6, 0)
             exponentials(state)
-            start_bank(g, 0, 1)
-            start_bank(g, 1, 1)
-            finish_coupling(g, 1, 0)
+            start_bank(7, 0)
+            start_bank(7, 1)
+            nc.scalar.copy(out=vision_rows[:, 4, :], in_=vision_bank[:])
+            finish_coupling(6, 1)
             normalise(state)
-            for t in range(ROWS):
-                weigh(g - 1, t, state)
-            finish_rows(g, 0, 1)
-            next_state = new_state(g)
-            place_coupling(next_state, 0)
-            finish_coupling(g, 1, 1)
-            finish_coupling(g, 0, 1)
-            state = next_state
-            place_coupling(state, 1)
-            gather_couplings(state)
-            finish_rows(g, 1, 1)
-            exponentials(state)
-            normalise(state)
-            for t in range(ROWS):
-                weigh(g, t, state)
+            sixth = new_state(3)
+            place_coupling(sixth, 0)
+            gather_couplings(sixth)
+            for t in range(2):
+                weigh(2, t, state)
+            finish_rows(7, 0)
+            finish_coupling(7, 1)
+            exponentials(sixth)
+            finish_coupling(7, 0)
+            seventh = new_state(4)
+            place_coupling(seventh, 0)
+            gather_couplings(seventh)
+            normalise(sixth)
+            weigh(3, 0, sixth)
+            finish_rows(7, 1)
+            exponentials(seventh)
+            normalise(seventh)
+            weigh(4, 0, seventh)

@@ -101,6 +101,10 @@ def tile_dynamicroutingfusion_pa_kernel(tc, text_feat, vision_proj, Wt, bt, out_
         for g in range(1, GROUPS):
             for first in range(0, GROUP_TILES[g], 2):
                 load_tokens(g, first, min(first + 2, GROUP_TILES[g]))
+        for g in (3, 4):
+            first, batches = FIRST_TILE[g] * BATCHES_PER_TILE, GROUP_TILES[g] * BATCHES_PER_TILE
+            rows = vision_proj[first : first + batches, :, :]
+            nc.sync.dma_start(out=vision_rows[:, g, :], in_=rows.to_broadcast([batches, P // batches, H]))
 
         ident = keep.tile([P, P], F32)
         make_identity(nc, ident[:])
@@ -423,7 +427,8 @@ def tile_dynamicroutingfusion_pa_kernel(tc, text_feat, vision_proj, Wt, bt, out_
                 exponentials(state)
                 start_bank(n + 1, 0)
                 start_bank(n + 1, 1)
-                vision_bank = spread_vision(g + 1)
+                if g == 1:
+                    vision_bank = spread_vision(2)
                 finish_rows(n + 1, 0)
                 finish_coupling(n, 1)
                 normalise(state)
@@ -437,7 +442,8 @@ def tile_dynamicroutingfusion_pa_kernel(tc, text_feat, vision_proj, Wt, bt, out_
                     transpose_x(n + 5)
                 next_state = new_state(g)
                 place_coupling(next_state, 0)
-                nc.scalar.copy(out=vision_rows[:, g + 1, :], in_=vision_bank[:])
+                if g == 1:
+                    nc.scalar.copy(out=vision_rows[:, 2, :], in_=vision_bank[:])
                 for t in range(2):
                     weigh(g - 1, t, state)
                 state = next_state
@@ -447,13 +453,11 @@ def tile_dynamicroutingfusion_pa_kernel(tc, text_feat, vision_proj, Wt, bt, out_
             finish_rows(6, 0)
             place_coupling(state, 1)
             gather_couplings(state)
-            vision_bank = spread_vision(4)
             finish_rows(6, 1)
             finish_coupling(6, 0)
             exponentials(state)
             start_bank(7, 0)
             start_bank(7, 1)
-            nc.scalar.copy(out=vision_rows[:, 4, :], in_=vision_bank[:])
             finish_coupling(6, 1)
             normalise(state)
             sixth = new_state(3)

from contextlib import ExitStack

import concourse.mybir as mybir
from concourse.masks import make_identity

F32 = mybir.dt.float32
BF16 = mybir.dt.bfloat16
U32 = mybir.dt.uint32
U8 = mybir.dt.uint8
FP8X4 = mybir.dt.float8_e4m3fn_x4
ALU = mybir.AluOpType
ACT = mybir.ActivationFunctionType
AXIS = mybir.AxisListType

P = 128
BATCH = 32
TOKENS = 32
H = 1024

K_PASS = 4 * P
PASSES = H // K_PASS
WORDS = K_PASS // 2
N_HALF = 512
HALVES = H // N_HALF

FIRST_TILES = 2
V_BIAS = tuple((n, 1) for n in range(8))
VS_PART = 320
VECTOR_WEIGHS = {(2, 0): H, (3, 0): 640, (4, 0): 640}
QUARTERS = P // BATCH
ROWS = 2
UNIT = ROWS * P
UNITS = H // UNIT
GROUP_TILES = (2, 2, 2, 1, 1)
GROUPS = len(GROUP_TILES)
TILE_LIST = [(g, t) for g, tiles in enumerate(GROUP_TILES) for t in range(tiles)]
FIRST_TILE = [sum(GROUP_TILES[:g]) for g in range(GROUPS)]
BATCHES_PER_TILE = P // TOKENS

FLOPS = 2 * BATCH * TOKENS * H * H


def tile_dynamicroutingfusion_pa_kernel(tc, text_feat, vision_proj, Wt, bt, out_0, out_1):
    nc = tc.nc

    def tokens_of(dram):
        flat = dram.flatten_outer_dims()
        views = []
        for g, tiles in enumerate(GROUP_TILES):
            first = FIRST_TILE[g] * P
            views.append(flat[first : first + tiles * P, :].rearrange("(p t) k -> p t k", t=tiles))
        return views

    x_dram = tokens_of(text_feat)
    proj_dram = tokens_of(out_0)
    weighted_dram = tokens_of(out_1)
    w_dram = Wt.rearrange("(g p t) k -> g p t k", p=P, t=ROWS)

    with ExitStack() as ctx:
        keep = ctx.enter_context(tc.tile_pool(name="keep", bufs=1))
        stage = ctx.enter_context(tc.tile_pool(name="stage", bufs=4))
        results = ctx.enter_context(tc.tile_pool(name="results", bufs=2 * ROWS))
        small = ctx.enter_context(tc.tile_pool(name="small", bufs=2))
        psum_t = ctx.enter_context(tc.psum_pool(name="psum_t", bufs=4))
        psum_acc = ctx.enter_context(tc.psum_pool(name="psum_acc", bufs=4))

        raw = {
            "x": keep.tile([P, len(TILE_LIST), H], BF16, name="x_raw"),
            "w": keep.tile([P, UNITS, ROWS, H], BF16, name="w_raw"),
        }
        codes = {
            "x": keep.tile([P, PASSES, H], U32, name="x_codes", align_bytes=64),
            "w": keep.tile([P, PASSES, H], U32, name="w_codes", align_bytes=64),
        }
        scales = {
            "x": keep.tile([P, PASSES, H], U8, name="x_scales", align_bytes=64),
            "w": keep.tile([P, PASSES, H], U8, name="w_scales", align_bytes=64),
        }
        vision_rows = keep.tile([P, GROUPS, H], BF16)
        vision_seed = keep.tile([P, H // QUARTERS], BF16)
        bias_seed = keep.tile([P, H], BF16)
        bias_rows = keep.tile([P, H], BF16)

        ones = keep.tile([P, P], BF16)
        nc.vector.memset(ones[:], 1.0)
        nc.vector.memset(bias_seed[:].bitcast(F32), 0.0)
        nc.sync.dma_start(
            out=vision_seed[:], in_=vision_proj.flatten_outer_dims().rearrange("b (q h) -> (b q) h", q=QUARTERS)
        )
        nc.sync.dma_start(out=bias_seed[0:1, :], in_=bt.unsqueeze(0))

        def load_tokens(g, first, end):
            tile = FIRST_TILE[g]
            nc.sync.dma_start(out=raw["x"][:, tile + first : tile + end, :], in_=x_dram[g][:, first:end, :])

        load_tokens(0, 0, FIRST_TILES)
        for u in range(UNITS):
            nc.sync.dma_start(out=raw["w"][:, u, :, :], in_=w_dram[u])
        if FIRST_TILES < GROUP_TILES[0]:
            load_tokens(0, FIRST_TILES, GROUP_TILES[0])
        for g in range(1, GROUPS):
            for first in range(0, GROUP_TILES[g], 2):
                load_tokens(g, first, min(first + 2, GROUP_TILES[g]))
        for g in (3, 4):
            first, batches = FIRST_TILE[g] * BATCHES_PER_TILE, GROUP_TILES[g] * BATCHES_PER_TILE
            rows = vision_proj[first : first + batches, :, :]
            nc.sync.dma_start(out=vision_rows[:, g, :], in_=rows.to_broadcast([batches, P // batches, H]))

        ident = keep.tile([P, P], F32)
        make_identity(nc, ident[:])
        quarter_of = ident[:].rearrange("p (b q) -> p q b", q=QUARTERS)
        pick = []
        for g, tiles in enumerate(GROUP_TILES):
            batches = tiles * BATCHES_PER_TILE
            first = FIRST_TILE[g] * BATCHES_PER_TILE
            pick.append(keep.tile([P, QUARTERS, batches, P // batches], BF16, name="pick", tag="pick%d" % g))
            nc.vector.tensor_copy(
                out=pick[g][:],
                in_=quarter_of[:, :, first : first + batches].unsqueeze(3).to_broadcast([P, QUARTERS, batches, P // batches]),
            )
        warm = keep.tile([P, 1], F32)
        nc.vector.memset(warm[:], 0.0)
        nc.scalar.activation(out=warm[:], in_=warm[:], func=ACT.Exp)
        same_batch = {}
        place_of = {}
        for tiles in sorted(set(GROUP_TILES)):
            batches = tiles * BATCHES_PER_TILE
            share = P // batches
            batch_of = keep.tile([P, batches], F32, name="batch_of", tag="batch_of%d" % tiles)
            nc.vector.tensor_reduce(
                out=batch_of[:], in_=ident[:].rearrange("p (b j) -> p b j", j=share), axis=AXIS.X, op=ALU.add
            )
            same_batch[tiles] = keep.tile([P, P], F32, name="same_batch", tag="same_batch%d" % tiles)
            nc.vector.tensor_copy(
                out=same_batch[tiles][:].rearrange("p (b j) -> p b j", j=share),
                in_=batch_of[:].unsqueeze(2).to_broadcast([P, batches, share]),
            )
            place_of[tiles] = keep.tile([P, share], F32, name="place_of", tag="place_of%d" % tiles)
            nc.vector.tensor_reduce(
                out=place_of[tiles][:], in_=ident[:].rearrange("p (b j) -> p j b", j=share), axis=AXIS.X, op=ALU.add
            )

        def pick_words(rows, c, u):
            return rows.bitcast(F32)[:, c * WORDS + u : (c + 1) * WORDS : 2]

        def transpose_tokens(g, t):
            bank = psum_t.tile([P, PASSES, 2, P], F32, tag="bank")
            for c in range(PASSES):
                for u in range(2):
                    nc.tensor.transpose(bank[:, c, u, :], pick_words(raw["x"][:, FIRST_TILE[g] + t, :], c, u), ident[:])
            return bank

        def transpose_weights(n, c):
            bank = psum_t.tile([P, 2, ROWS, P], F32, tag="bank")
            for t in range(ROWS):
                for u in range(2):
                    nc.tensor.transpose(bank[:, u, t, :], pick_words(raw["w"][:, n, t, :], c, u), ident[:])
            return bank

        def regroup_tokens(bank, copy):
            grouped = stage.tile([P, UNIT * 4], BF16, align_bytes=64, tag="grouped")
            out = grouped[:].bitcast(F32).rearrange("p (c r u) -> p c r u", c=PASSES, u=2)
            copy(out=out, in_=bank[:].rearrange("p c u r -> p c r u"))
            return grouped

        def regroup_weights(bank, copy):
            grouped = stage.tile([P, UNIT * 4], BF16, align_bytes=64, tag="grouped")
            out = grouped[:].bitcast(F32).rearrange("p (r t u) -> p r t u", t=ROWS, u=2)
            copy(out=out, in_=bank[:].rearrange("p u t r -> p r t u"))
            return grouped

        def quantise(operand, c, first, width, in_):
            nc.vector.quantize_mx(
                out=codes[operand][:, c, first : first + width].bitcast(FP8X4),
                scales=scales[operand][:, c, first : first + width],
                in_=in_,
            )

        def spread_vision(g):
            bank = psum_t.tile([P, H], BF16, tag="bank")
            width = H // QUARTERS
            for q in range(QUARTERS):
                lhsT = pick[g][:, q, :, :].rearrange("p b j -> p (b j)")
                cols = slice(q * width, (q + 1) * width)
                nc.tensor.matmul(out=bank[:, cols], lhsT=lhsT, rhs=vision_seed[:], start=True, stop=True)
            return bank

        def spread_bias():
            bank = psum_t.tile([P, H], BF16, tag="bank")
            for half in range(HALVES):
                cols = slice(half * N_HALF, (half + 1) * N_HALF)
                nc.tensor.matmul(out=bank[:, cols], lhsT=ones[:], rhs=bias_seed[:, cols], start=True, stop=True)
            return bank

        def multiply(g, half, t):
            first = (FIRST_TILE[g] + t) * P
            acc = psum_acc.tile([P, N_HALF], F32)
            for c in range(PASSES):
                nc.tensor.matmul_mx(
                    out=acc[:],
                    lhsT=codes["x"][:, c, first : first + P].bitcast(FP8X4),
                    lhsT_scale=scales["x"][:, c, first : first + P],
                    rhs=codes["w"][:, c, half * N_HALF : (half + 1) * N_HALF].bitcast(FP8X4),
                    rhs_scale=scales["w"][:, c, half * N_HALF : (half + 1) * N_HALF],
                    start=(c == 0),
                    stop=(c == PASSES - 1),
                )
            return acc

        def agree(g, half, t, acc, coupling_parts):
            cols = slice(half * N_HALF, (half + 1) * N_HALF)
            product = stage.tile([P, N_HALF], F32, tag="product")
            nc.vector.scalar_tensor_tensor(
                out=product[:],
                in0=acc[:],
                scalar=2.0,
                in1=vision_rows[:, g, cols],
                op0=ALU.mult,
                op1=ALU.mult,
                accum_out=coupling_parts[:, half, t : t + 1],
            )

        def add_bias(g, half, t, acc, proj, by_vector):
            cols = slice(half * N_HALF, (half + 1) * N_HALF)
            if by_vector:
                nc.vector.tensor_tensor(out=proj[:, cols], in0=acc[:], in1=bias_rows[:, cols], op=ALU.add)
            else:
                bare = stage.tile([P, N_HALF], F32, tag="bare")
                nc.scalar.copy(out=bare[:], in_=acc[:])
                nc.gpsimd.tensor_tensor(out=proj[:, cols], in0=bare[:], in1=bias_rows[:, cols], op=ALU.add)
        def new_state(g):
            tiles = GROUP_TILES[g]
            return {
                "group": g,
                "tiles": tiles,
                "coupling": small.tile([P, tiles], F32, name="coupling", tag="coupling"),
                "spread": small.tile([P, tiles, TOKENS // tiles], F32, name="spread", tag="spread"),
            }

        def place_coupling(state, t):
            parts = coupling_parts[state["group"]]
            coupling = state["coupling"][:, t : t + 1]
            nc.scalar.activation(
                out=coupling, in_=parts[:, 0, t : t + 1], func=ACT.Identity, bias=parts[:, 1, t : t + 1]
            )
            nc.scalar.activation(
                out=state["spread"][:, t, :], in_=place_of[state["tiles"]][:], func=ACT.Copy, scale=coupling
            )

        def gather_couplings(state):
            state["batch_couplings"] = psum_t.tile([P, TOKENS], F32, name="batch_couplings", tag="bank")
            nc.tensor.matmul(
                out=state["batch_couplings"][:],
                lhsT=same_batch[state["tiles"]][:],
                rhs=state["spread"][:].rearrange("p t j -> p (t j)"),
                start=True,
                stop=True,
            )

        def exponentials(state):
            minus_max = small.tile([P, 1], F32, tag="minus_max")
            nc.vector.tensor_reduce(
                out=minus_max[:], in_=state["batch_couplings"][:], axis=AXIS.X, op=ALU.max, negate=True
            )
            exp_all = small.tile([P, TOKENS], F32, tag="exp_all")
            exp_sum = small.tile([P, 1], F32, tag="exp_sum")
            nc.scalar.activation(
                out=exp_all[:],
                in_=state["batch_couplings"][:],
                func=ACT.Exp,
                bias=minus_max[:],
                scale=1.0,
                accum_out=exp_sum[:],
            )
            exp_own = small.tile([P, state["tiles"]], F32, name="exp_own", tag="exp_own%d" % state["tiles"])
            nc.scalar.activation(out=exp_own[:], in_=state["coupling"][:], func=ACT.Exp, bias=minus_max[:], scale=1.0)
            state["exp_sum"] = exp_sum
            state["exp_own"] = exp_own

        def normalise(state):
            inverse_sum = small.tile([P, 1], F32, tag="inverse_sum")
            nc.vector.reciprocal(out=inverse_sum[:], in_=state["exp_sum"][:])
            routing = small.tile([P, state["tiles"]], F32, name="routing", tag="routing%d" % state["tiles"])
            nc.scalar.activation(out=routing[:], in_=state["exp_own"][:], func=ACT.Copy, scale=inverse_sum[:])
            state["inverse_sum"] = inverse_sum
            state["routing"] = routing

        def weigh(g, t, state):
            weighted = results.tile([P, H], F32, name="weighted", tag="weighted", bufs=5)
            by_vector = VECTOR_WEIGHS.get((g, t), 0)
            if by_vector > 0:
                nc.vector.tensor_scalar(
                    out=weighted[:, 0:by_vector],
                    in0=vision_rows[:, g, 0:by_vector],
                    scalar1=state["exp_own"][:, t : t + 1],
                    scalar2=state["inverse_sum"][:, 0:1],
                    op0=ALU.mult,
                    op1=ALU.mult,
                )
            by_scalar = H if by_vector > 0 else VS_PART
            if by_vector < by_scalar:
                nc.scalar.activation(
                    out=weighted[:, by_vector:by_scalar],
                    in_=vision_rows[:, g, by_vector:by_scalar],
                    func=ACT.Copy,
                    scale=state["routing"][:, t : t + 1],
                )
            if by_scalar < H:
                nc.gpsimd.tensor_scalar(
                    out=weighted[:, by_scalar:H],
                    in0=vision_rows[:, g, by_scalar:H],
                    scalar1=state["exp_own"][:, t : t + 1],
                    scalar2=state["inverse_sum"][:, 0:1],
                    op0=ALU.mult,
                    op1=ALU.mult,
                )
            nc.sync.dma_start(out=weighted_dram[g][:, t, :], in_=weighted[:])

        proj_tiles = {}
        accs = {}
        coupling_parts = [
            small.tile([P, HALVES, tiles], F32, name="coupling_parts", tag="coupling_parts%d" % g, bufs=1)
            for g, tiles in enumerate(GROUP_TILES)
        ]

        def start_bank(n, half):
            accs[n, half] = multiply(TILE_LIST[n][0], half, TILE_LIST[n][1])

        def finish_coupling(n, half):
            g, t = TILE_LIST[n]
            agree(g, half, t, accs[n, half], coupling_parts[g])

        def finish_rows(n, half):
            g, t = TILE_LIST[n]
            if n not in proj_tiles:
                proj_tiles[n] = results.tile([P, H], F32, name="proj", tag="proj", bufs=4)
            add_bias(g, half, t, accs[n, half], proj_tiles[n], (n, half) in V_BIAS)
            if half == HALVES - 1:
                nc.sync.dma_start(out=proj_dram[g][:, t, :], in_=proj_tiles[n][:])

        banks = {}
        grouped = {}

        def transpose_x(n):
            banks[n] = transpose_tokens(*TILE_LIST[n])

        def regroup_x(n, copy):
            grouped[n] = regroup_tokens(banks[n], copy)

        def quantise_x(n):
            for c in range(PASSES):
                quantise("x", c, n * P, P, grouped[n][:, c * P * 4 : (c + 1) * P * 4])

        def transpose_w(n):
            for c in range(PASSES):
                banks["w", n, c] = transpose_weights(n, c)

        def regroup_w(n, copies):
            for c in range(PASSES):
                grouped["w", n, c] = regroup_weights(banks["w", n, c], copies[c])

        def quantise_w(n):
            for c in range(PASSES):
                quantise("w", c, n * UNIT, UNIT, grouped["w", n, c][:])

        on_scalar = (nc.scalar.copy, nc.scalar.copy)
        on_both = (nc.scalar.copy, nc.vector.tensor_copy)
        with tc.manual_schedule():
            vision_bank = spread_vision(0)
            nc.scalar.copy(out=vision_rows[:, 0, :], in_=vision_bank[:])
            transpose_x(0)
            transpose_x(1)
            regroup_x(0, nc.scalar.copy)
            regroup_x(1, nc.vector.tensor_copy)
            quantise_x(0)
            quantise_x(1)
            transpose_w(0)
            regroup_w(0, on_both)
            quantise_w(0)
            transpose_w(1)
            regroup_w(1, on_both)
            quantise_w(1)
            transpose_w(2)
            regroup_w(2, on_scalar)
            transpose_w(3)
            quantise_w(2)
            bias_bank = spread_bias()
            start_bank(0, 0)
            start_bank(1, 0)
            regroup_w(3, on_scalar)
            nc.scalar.copy(out=bias_rows[:], in_=bias_bank[:])
            quantise_w(3)
            start_bank(0, 1)
            transpose_x(2)
            transpose_x(3)
            start_bank(1, 1)
            vision_bank = spread_vision(1)
            finish_coupling(0, 0)
            finish_rows(0, 0)
            finish_coupling(1, 0)
            finish_rows(0, 1)
            regroup_x(2, nc.scalar.copy)
            regroup_x(3, nc.scalar.copy)
            finish_coupling(0, 1)
            quantise_x(2)
            quantise_x(3)
            finish_rows(1, 0)
            nc.scalar.copy(out=vision_rows[:, 1, :], in_=vision_bank[:])
            finish_rows(1, 1)
            start_bank(2, 0)
            state = new_state(0)
            place_coupling(state, 0)
            finish_coupling(1, 1)
            start_bank(2, 1)
            transpose_x(4)
            transpose_x(5)

            for g in (1, 2):
                n = 2 * g
                finish_rows(n, 0)
                place_coupling(state, 1)
                gather_couplings(state)
                finish_rows(n, 1)
                finish_coupling(n, 0)
                regroup_x(n + 2, nc.scalar.copy)
                regroup_x(n + 3, nc.scalar.copy)
                exponentials(state)
                start_bank(n + 1, 0)
                start_bank(n + 1, 1)
                if g == 1:
                    vision_bank = spread_vision(2)
                finish_rows(n + 1, 0)
                finish_coupling(n, 1)
                normalise(state)
                quantise_x(n + 2)
                quantise_x(n + 3)
                start_bank(n + 2, 0)
                finish_rows(n + 1, 1)
                start_bank(n + 2, 1)
                if g == 1:
                    transpose_x(n + 4)
                    transpose_x(n + 5)
                next_state = new_state(g)
                place_coupling(next_state, 0)
                if g == 1:
                    nc.scalar.copy(out=vision_rows[:, 2, :], in_=vision_bank[:])
                for t in range(2):
                    weigh(g - 1, t, state)
                state = next_state
                finish_coupling(n + 1, 0)
                finish_coupling(n + 1, 1)

            finish_rows(6, 0)
            place_coupling(state, 1)
            gather_couplings(state)
            finish_rows(6, 1)
            finish_coupling(6, 0)
            exponentials(state)
            start_bank(7, 0)
            start_bank(7, 1)
            finish_coupling(6, 1)
            normalise(state)
            sixth = new_state(3)
            place_coupling(sixth, 0)
            gather_couplings(sixth)
            for t in range(2):
                weigh(2, t, state)
            finish_rows(7, 0)
            finish_coupling(7, 1)
            exponentials(sixth)
            finish_coupling(7, 0)
            seventh = new_state(4)
            place_coupling(seventh, 0)
            gather_couplings(seventh)
            normalise(sixth)
            weigh(3, 0, sixth)
            finish_rows(7, 1)
            exponentials(seventh)
            normalise(seventh)
            weigh(4, 0, seventh)
